import numpy as np
import ml_dtypes


def mxq(x, axis, fmt="e4m3"):
    dtype, down = {"e4m3": (ml_dtypes.float8_e4m3fn, 7), "e5m2": (ml_dtypes.float8_e5m2, 14)}[fmt]
    v = np.moveaxis(np.asarray(x, np.float32).astype(ml_dtypes.bfloat16).astype(np.float64), axis, -1)
    blocks = v.reshape(v.shape[:-1] + (-1, 32))
    amax = np.abs(blocks).max(-1, keepdims=True)
    byte = np.maximum(np.where(amax > 0, np.frexp(amax)[1] - 1 + 127, 0) - down, 1)
    scale = np.exp2(byte - 127.0)
    codes = (blocks / scale).astype(np.float32).astype(dtype).astype(np.float64)
    return np.moveaxis((codes * scale).reshape(v.shape), -1, axis)


WIDE = False


def mx_kscale(k):
    if not WIDE:
        return np.ones(k)
    levels = np.array([10, -10, 5, -5, 0])
    a = np.random.permutation(np.resize(levels, k // 512 * 4)).reshape(k // 512, 4)
    idx = np.arange(k)
    return np.exp2(a[idx // 512, idx % 128 // 32])


BF16 = ml_dtypes.bfloat16


def bf(x):
    return np.asarray(x, np.float32).astype(BF16)


def f64(x):
    return np.asarray(x).astype(np.float64)


B, S, D, H, W, F = 1, 1536, 1024, 8, 512, 2048
EPS = 1e-5


def erf(v):
    a = np.minimum(np.abs(v), 6.0)
    a2 = 2.0 * a * a
    term = a * 1.0
    total = a * 1.0
    for n in range(1, 100):
        term = term * a2 / (2 * n + 1)
        total = total + term
    return np.sign(v) * (2.0 / np.sqrt(np.pi)) * np.exp(-a * a) * total


def gelu_erf(v):
    return 0.5 * v * (1.0 + erf(v / np.sqrt(2.0)))


def setup_inputs():
    s = mx_kscale(D)
    return {"x": bf(np.random.standard_normal((B, S, D))),
            "o_heads": bf(np.random.standard_normal((B, S, D)) * 0.35 * s),
            "Wo": bf(np.random.standard_normal((D, D)) * 2.0 / np.sqrt(D) / s[:, None]),
            "bo": bf(np.random.standard_normal(D) * 0.1),
            "gamma": bf(1.0 + 0.1 * np.random.standard_normal(D)),
            "beta": bf(np.random.standard_normal(D) * 0.1),
            "W1": bf(np.random.standard_normal((D, F)) / np.sqrt(D)),
            "b1": bf(np.random.standard_normal(F) * 0.1)}


def reference(x, o_heads, Wo, bo, gamma, beta, W1, b1):
    attn = (mxq(f64(o_heads), 2, "e4m3") @ mxq(f64(Wo), 0, "e4m3")) + f64(bo)
    r = f64(x) + attn
    mu = r.mean(-1, keepdims=True)
    var = ((r - mu) ** 2).mean(-1, keepdims=True)
    xn = (r - mu) / np.sqrt(var + EPS) * f64(gamma) + f64(beta)
    h = gelu_erf((mxq(xn, 2, "e4m3") @ mxq(f64(W1), 0, "e4m3")) + f64(b1))
    return xn, h

@@ -1,0 +1,273 @@
+from contextlib import ExitStack
+
+import concourse.mybir as mybir
+from concourse.masks import make_identity
+
+F32 = mybir.dt.float32
+BF16 = mybir.dt.bfloat16
+U32 = mybir.dt.uint32
+U8 = mybir.dt.uint8
+FP8X4 = mybir.dt.float8_e4m3fn_x4
+ALU = mybir.AluOpType
+ACT = mybir.ActivationFunctionType
+
+S, D, F = 1536, 1024, 2048
+EPS = 1e-5
+P = 128
+PACK = 4
+K_PASS = P * PACK
+PASSES = D // K_PASS
+N_TILE = 512
+TOKEN_TILES = S // P
+LOAD_GROUP = 4
+HALF = 2 * N_TILE
+LAG = 2
+
+FLOPS = 2 * S * D * D + 2 * S * D * F
+
+
+def tile_swablock_pb_kernel(tc, x, o_heads, Wo, bo, gamma, beta, W1, b1, out_0, out_1):
+    nc = tc.nc
+    x_rows = x.flatten_outer_dims().rearrange("(p n) d -> p n d", n=TOKEN_TILES)
+    o_rows = o_heads.flatten_outer_dims().rearrange("(p n) d -> p n d", n=TOKEN_TILES)
+    xn_rows = out_0.flatten_outer_dims().rearrange("(p n) d -> p n d", n=TOKEN_TILES)
+    h_rows = out_1.flatten_outer_dims().rearrange("(p n) f -> p n f", n=TOKEN_TILES)
+
+    with ExitStack() as ctx:
+        keep = ctx.enter_context(tc.tile_pool(name="keep", bufs=1))
+        work = ctx.enter_context(tc.tile_pool(name="work", bufs=2))
+        psum = ctx.enter_context(tc.psum_pool(name="psum", bufs=2))
+
+        o_all = keep.tile([P, TOKEN_TILES, D], BF16)
+        x_all = keep.tile([P, TOKEN_TILES, D], BF16)
+        wo_raw = keep.tile([P, PASSES, PACK, D], BF16)
+        w1_raw = keep.tile([P, PASSES, PACK, F], BF16)
+
+        def load_tokens(dst, src, first):
+            group = slice(first, first + LOAD_GROUP)
+            nc.sync.dma_start(out=dst[:, group, :], in_=src[:, group, :])
+
+        load_tokens(o_all, o_rows, 0)
+        for g in range(PASSES):
+            for u in range(2):
+                k0 = g * K_PASS + u * 2 * P
+                nc.sync.dma_start(
+                    out=wo_raw[:, g, 2 * u : 2 * u + 2, :],
+                    in_=Wo[k0 : k0 + 2 * P, :].rearrange("(q e) c -> q e c", e=2),
+                )
+        load_tokens(x_all, x_rows, 0)
+        for half in range(F // HALF):
+            cols = slice(half * HALF, (half + 1) * HALF)
+            for g in range(PASSES):
+                nc.sync.dma_start(
+                    out=w1_raw[:, g, :, cols],
+                    in_=W1[g * K_PASS : (g + 1) * K_PASS, cols].rearrange("(t p) n -> p t n", p=P),
+                )
+        for first in range(LOAD_GROUP, TOKEN_TILES, LOAD_GROUP):
+            load_tokens(o_all, o_rows, first)
+            load_tokens(x_all, x_rows, first)
+
+        ident_f32 = keep.tile([P, P], F32)
+        make_identity(nc, ident_f32[:])
+        ident_bf16 = keep.tile([P, P], BF16)
+        make_identity(nc, ident_bf16[:])
+        neg_half = keep.tile([P, 1], F32)
+        nc.gpsimd.memset(neg_half[:], -0.5)
+
+        vector_rows = keep.tile([P, D], BF16)
+        nc.vector.memset(vector_rows[:], 0.0)
+        nc.scalar.dma_start(out=vector_rows[0:1, :], in_=bo.unsqueeze(0))
+        nc.scalar.dma_start(out=vector_rows[1:2, :], in_=gamma.unsqueeze(0))
+        nc.scalar.dma_start(out=vector_rows[2:3, :], in_=beta.unsqueeze(0))
+        nc.scalar.dma_start(out=vector_rows[3:5, :], in_=b1.rearrange("(a c) -> a c", a=2))
+        spread = keep.tile([P, 5 * D], BF16)
+
+        def spread_row(j):
+            for n in range(D // N_TILE):
+                cols = slice(n * N_TILE, (n + 1) * N_TILE)
+                acc = psum.tile([P, N_TILE], F32, tag="acc2", bufs=4)
+                nc.tensor.matmul(
+                    out=acc[:],
+                    lhsT=ident_bf16[:, j : j + 1].to_broadcast([P, P]),
+                    rhs=vector_rows[:, cols],
+                    start=True,
+                    stop=True,
+                )
+                nc.scalar.copy(out=spread[:, j * D + n * N_TILE : j * D + (n + 1) * N_TILE], in_=acc[:])
+
+        bo_all = spread[:, 0:D]
+        gamma_all = spread[:, D : 2 * D]
+        beta_all = spread[:, 2 * D : 3 * D]
+        b1_all = spread[:, 3 * D : 5 * D]
+
+        wo_codes = keep.tile([P, PASSES, D], U32, align_bytes=64)
+        wo_scales = keep.tile([P, PASSES, D], U8, align_bytes=64)
+        w1_codes = keep.tile([P, PASSES, F], U32, align_bytes=64)
+        w1_scales = keep.tile([P, PASSES, F], U8, align_bytes=64)
+
+        def quantise_weights(copy, raw, codes, scales, g, n):
+            cols = slice(n * N_TILE, (n + 1) * N_TILE)
+            grouped = work.tile([P, N_TILE * PACK], BF16, align_bytes=64, tag="w_grouped", bufs=3)
+            copy(
+                out=grouped[:].rearrange("p (c i t) -> p c t i", i=4, t=PACK),
+                in_=raw[:, g, :, cols].rearrange("p t (c i) -> p c t i", i=4),
+            )
+            nc.vector.quantize_mx(
+                out=codes[:, g, cols].bitcast(FP8X4), scales=scales[:, g, cols], in_=grouped[:]
+            )
+
+        def copy_engine(chunk):
+            return nc.vector.tensor_copy if chunk % 2 == 0 else nc.scalar.copy
+
+        biased = {}
+        heads = {}
+        normed = {}
+
+        def add_bias(i):
+            xb = work.tile([P, D], F32, tag="xb", bufs=3)
+            nc.gpsimd.tensor_tensor(out=xb[:], in0=x_all[:, i, :], in1=bo_all, op=ALU.add)
+            biased[i] = xb
+
+        def quantise_heads(i):
+            words = o_all[:, i, :].bitcast(F32)
+            flipped = psum.tile([P, PASSES * 2, P], F32, tag="flipped", bufs=2)
+            for a in range(PASSES * 2):
+                nc.tensor.transpose(flipped[:, a, :], words[:, a * P : (a + 1) * P], ident_f32[:])
+            grouped = work.tile([P, D], BF16, align_bytes=64, tag="o_grouped", bufs=2)
+            nc.scalar.copy(
+                out=grouped[:].bitcast(F32).rearrange("p (g r u) -> p g r u", g=PASSES, u=2),
+                in_=flipped[:].rearrange("p (g u) r -> p g r u", u=2),
+            )
+            codes = work.tile([P, PASSES * P], U32, align_bytes=64, tag="o_codes", bufs=3)
+            scales = work.tile([P, PASSES * P], U8, align_bytes=64, tag="o_scales", bufs=3)
+            nc.vector.quantize_mx(out=codes[:].bitcast(FP8X4), scales=scales[:], in_=grouped[:])
+            heads[i] = (codes, scales)
+
+        def project_and_norm(i):
+            codes, scales = heads.pop(i)
+            xb = biased.pop(i)
+            residual = work.tile([P, D], F32, tag="residual", bufs=2)
+            row_sums = work.tile([P, D // N_TILE], F32, tag="row_sums", bufs=3)
+            for n in range(D // N_TILE):
+                cols = slice(n * N_TILE, (n + 1) * N_TILE)
+                acc = psum.tile([P, N_TILE], F32, tag="acc1", bufs=2)
+                for g in range(PASSES):
+                    toks = slice(g * P, (g + 1) * P)
+                    nc.tensor.matmul_mx(
+                        out=acc[:],
+                        lhsT=codes[:, toks].bitcast(FP8X4),
+                        lhsT_scale=scales[:, toks],
+                        rhs=wo_codes[:, g, cols].bitcast(FP8X4),
+                        rhs_scale=wo_scales[:, g, cols],
+                        start=(g == 0),
+                        stop=(g == PASSES - 1),
+                    )
+                nc.vector.scalar_tensor_tensor(
+                    out=residual[:, cols],
+                    in0=acc[:],
+                    scalar=1.0,
+                    in1=xb[:, cols],
+                    op0=ALU.mult,
+                    op1=ALU.add,
+                    accum_out=row_sums[:, n : n + 1],
+                )
+            neg_mean = work.tile([P, 1], F32, tag="neg_mean", bufs=3)
+            nc.vector.tensor_scalar(
+                out=neg_mean[:],
+                in0=row_sums[:, 0:1],
+                scalar1=row_sums[:, 1:2],
+                scalar2=-1.0 / D,
+                op0=ALU.add,
+                op1=ALU.mult,
+            )
+            squares = work.tile([P, D], BF16, tag="squares", bufs=2)
+            sum_sq = work.tile([P, 1], F32, tag="sum_sq", bufs=3)
+            nc.scalar.activation(
+                out=squares[:], in_=residual[:], func=ACT.Square, bias=neg_mean[:], scale=1.0,
+                accum_out=sum_sq[:],
+            )
+            centred = work.tile([P, D], F32, tag="centred", bufs=2)
+            nc.vector.scalar_tensor_tensor(
+                out=centred[:], in0=residual[:], scalar=neg_mean[:], in1=gamma_all,
+                op0=ALU.add, op1=ALU.mult,
+            )
+            var_eps = work.tile([P, 1], F32, tag="var_eps", bufs=3)
+            nc.gpsimd.tensor_scalar(
+                out=var_eps[:], in0=sum_sq[:], scalar1=1.0 / D, scalar2=EPS, op0=ALU.mult, op1=ALU.add
+            )
+            rstd = work.tile([P, 1], F32, tag="rstd", bufs=3)
+            nc.gpsimd.tensor_tensor(out=rstd[:], in0=var_eps[:], in1=neg_half[:], op=ALU.pow)
+            xn = work.tile([P, D], F32, tag="xn", bufs=3)
+            nc.vector.scalar_tensor_tensor(
+                out=xn[:], in0=centred[:], scalar=rstd[:], in1=beta_all, op0=ALU.mult, op1=ALU.add
+            )
+            nc.sync.dma_start(out=xn_rows[:, i, :], in_=xn[:])
+
+            grouped = work.tile([P, D], BF16, align_bytes=64, tag="xn_grouped", bufs=2)
+            for g in range(PASSES):
+                flipped = psum.tile([P, PACK, P], F32, tag="flipped", bufs=2)
+                for t in range(PACK):
+                    k0 = g * K_PASS + t * P
+                    nc.tensor.transpose(flipped[:, t, :], xn[:, k0 : k0 + P], ident_f32[:])
+                nc.scalar.copy(
+                    out=grouped[:, g * K_PASS : (g + 1) * K_PASS].rearrange("p (r t) -> p r t", t=PACK),
+                    in_=flipped[:].rearrange("p t r -> p r t"),
+                )
+            xn_codes = work.tile([P, PASSES * P], U32, align_bytes=64, tag="xn_codes", bufs=LAG + 2)
+            xn_scales = work.tile([P, PASSES * P], U8, align_bytes=64, tag="xn_scales", bufs=LAG + 2)
+            nc.vector.quantize_mx(out=xn_codes[:].bitcast(FP8X4), scales=xn_scales[:], in_=grouped[:])
+            normed[i] = (xn_codes, xn_scales)
+
+        def hidden_layer(i):
+            codes, scales = normed.pop(i)
+            for half in range(F // HALF):
+                hidden = work.tile([P, HALF], F32, tag="hidden", bufs=4)
+                for n in range(HALF // N_TILE):
+                    cols = slice(half * HALF + n * N_TILE, half * HALF + (n + 1) * N_TILE)
+                    acc = psum.tile([P, N_TILE], F32, tag="acc2", bufs=4)
+                    for g in range(PASSES):
+                        toks = slice(g * P, (g + 1) * P)
+                        nc.tensor.matmul_mx(
+                            out=acc[:],
+                            lhsT=codes[:, toks].bitcast(FP8X4),
+                            lhsT_scale=scales[:, toks],
+                            rhs=w1_codes[:, g, cols].bitcast(FP8X4),
+                            rhs_scale=w1_scales[:, g, cols],
+                            start=(g == 0),
+                            stop=(g == PASSES - 1),
+                        )
+                    nc.vector.tensor_tensor(
+                        out=hidden[:, n * N_TILE : (n + 1) * N_TILE], in0=acc[:], in1=b1_all[:, cols],
+                        op=ALU.add,
+                    )
+                nc.scalar.activation(out=hidden[:], in_=hidden[:], func=ACT.Gelu)
+                nc.sync.dma_start(out=h_rows[:, i, half * HALF : (half + 1) * HALF], in_=hidden[:])
+
+        spread_row(0)
+        quantise_heads(0)
+        add_bias(0)
+        chunk = 0
+        for n in range(D // N_TILE):
+            for g in range(PASSES):
+                quantise_weights(copy_engine(chunk), wo_raw, wo_codes, wo_scales, g, n)
+                chunk += 1
+        spread_row(1)
+        spread_row(2)
+
+        w1_chunks = [(g, n) for n in range(F // N_TILE) for g in range(PASSES)]
+        per_step = len(w1_chunks) // LAG
+        for step in range(TOKEN_TILES + LAG):
+            if step + 1 < TOKEN_TILES:
+                quantise_heads(step + 1)
+                add_bias(step + 1)
+            if step < TOKEN_TILES:
+                project_and_norm(step)
+            if step < LAG:
+                for g, n in w1_chunks[step * per_step : (step + 1) * per_step]:
+                    quantise_weights(copy_engine(chunk), w1_raw, w1_codes, w1_scales, g, n)
+                    chunk += 1
+            if step == 0:
+                spread_row(3)
+                spread_row(4)
+            if step >= LAG:
+                hidden_layer(step - LAG)

@@ -125,7 +125,7 @@ def tile_swablock_pb_kernel(tc, x, o_heads, Wo, bo, gamma, beta, W1, b1, out_0, 
 
         def add_bias(i):
             xb = work.tile([P, D], F32, tag="xb", bufs=3)
-            nc.gpsimd.tensor_tensor(out=xb[:], in0=x_all[:, i, :], in1=bo_all, op=ALU.add)
+            nc.vector.tensor_tensor(out=xb[:], in0=x_all[:, i, :], in1=bo_all, op=ALU.add)
             biased[i] = xb
 
         def quantise_heads(i):

@@ -18,61 +18,34 @@ PACK = 4
 K_PASS = P * PACK
 PASSES = D // K_PASS
 N_TILE = 512
-TOKEN_TILES = S // P
-LOAD_GROUP = 4
 HALF = 2 * N_TILE
+TOKEN_TILES = S // P
 LAG = 2
+
+assert LAG * HALF == F
 
 FLOPS = 2 * S * D * D + 2 * S * D * F
 
 
 def tile_swablock_pb_kernel(tc, x, o_heads, Wo, bo, gamma, beta, W1, b1, out_0, out_1):
     nc = tc.nc
-    x_rows = x.flatten_outer_dims().rearrange("(p n) d -> p n d", n=TOKEN_TILES)
-    o_rows = o_heads.flatten_outer_dims().rearrange("(p n) d -> p n d", n=TOKEN_TILES)
-    xn_rows = out_0.flatten_outer_dims().rearrange("(p n) d -> p n d", n=TOKEN_TILES)
-    h_rows = out_1.flatten_outer_dims().rearrange("(p n) f -> p n f", n=TOKEN_TILES)
+    x_tiles = x.flatten_outer_dims().rearrange("(n p) d -> n p d", p=P)
+    o_tiles = o_heads.flatten_outer_dims().rearrange("(n p) d -> n p d", p=P)
+    xn_tiles = out_0.flatten_outer_dims().rearrange("(n p) d -> n p d", p=P)
+    h_tiles = out_1.flatten_outer_dims().rearrange("(n p) f -> n p f", p=P)
 
     with ExitStack() as ctx:
+        ctx.enter_context(tc.manual_schedule())
         keep = ctx.enter_context(tc.tile_pool(name="keep", bufs=1))
         work = ctx.enter_context(tc.tile_pool(name="work", bufs=2))
-        psum = ctx.enter_context(tc.psum_pool(name="psum", bufs=2))
-
-        o_all = keep.tile([P, TOKEN_TILES, D], BF16)
-        x_all = keep.tile([P, TOKEN_TILES, D], BF16)
-        wo_raw = keep.tile([P, PASSES, PACK, D], BF16)
-        w1_raw = keep.tile([P, PASSES, PACK, F], BF16)
-
-        def load_tokens(dst, src, first):
-            group = slice(first, first + LOAD_GROUP)
-            nc.sync.dma_start(out=dst[:, group, :], in_=src[:, group, :])
-
-        load_tokens(o_all, o_rows, 0)
-        for g in range(PASSES):
-            for u in range(2):
-                k0 = g * K_PASS + u * 2 * P
-                nc.sync.dma_start(
-                    out=wo_raw[:, g, 2 * u : 2 * u + 2, :],
-                    in_=Wo[k0 : k0 + 2 * P, :].rearrange("(q e) c -> q e c", e=2),
-                )
-        load_tokens(x_all, x_rows, 0)
-        for half in range(F // HALF):
-            cols = slice(half * HALF, (half + 1) * HALF)
-            for g in range(PASSES):
-                nc.sync.dma_start(
-                    out=w1_raw[:, g, :, cols],
-                    in_=W1[g * K_PASS : (g + 1) * K_PASS, cols].rearrange("(t p) n -> p t n", p=P),
-                )
-        for first in range(LOAD_GROUP, TOKEN_TILES, LOAD_GROUP):
-            load_tokens(o_all, o_rows, first)
-            load_tokens(x_all, x_rows, first)
+        psum = ctx.enter_context(tc.psum_pool(name="psum", bufs=4))
 
         ident_f32 = keep.tile([P, P], F32)
         make_identity(nc, ident_f32[:])
         ident_bf16 = keep.tile([P, P], BF16)
         make_identity(nc, ident_bf16[:])
         neg_half = keep.tile([P, 1], F32)
-        nc.gpsimd.memset(neg_half[:], -0.5)
+        nc.vector.memset(neg_half[:], -0.5)
 
         vector_rows = keep.tile([P, D], BF16)
         nc.vector.memset(vector_rows[:], 0.0)
@@ -80,132 +53,209 @@ def tile_swablock_pb_kernel(tc, x, o_heads, Wo, bo, gamma, beta, W1, b1, out_0, 
         nc.scalar.dma_start(out=vector_rows[1:2, :], in_=gamma.unsqueeze(0))
         nc.scalar.dma_start(out=vector_rows[2:3, :], in_=beta.unsqueeze(0))
         nc.scalar.dma_start(out=vector_rows[3:5, :], in_=b1.rearrange("(a c) -> a c", a=2))
-        spread = keep.tile([P, 5 * D], BF16)
+        warm = keep.tile([P, 1], F32)
+        nc.scalar.activation(out=warm[:], in_=neg_half[:], func=ACT.Gelu)
 
-        def spread_row(j):
+        def row_selector(j):
+            return ident_bf16[:, j : j + 1].to_broadcast([P, P])
+
+        gamma_all = keep.tile([P, D], BF16)
+        beta_all = keep.tile([P, D], BF16)
+        b1_all = keep.tile([P, F], BF16)
+
+        def spread_row(j, copy, dst):
             for n in range(D // N_TILE):
                 cols = slice(n * N_TILE, (n + 1) * N_TILE)
-                acc = psum.tile([P, N_TILE], F32, tag="acc2", bufs=4)
-                nc.tensor.matmul(
-                    out=acc[:],
-                    lhsT=ident_bf16[:, j : j + 1].to_broadcast([P, P]),
-                    rhs=vector_rows[:, cols],
-                    start=True,
-                    stop=True,
-                )
-                nc.scalar.copy(out=spread[:, j * D + n * N_TILE : j * D + (n + 1) * N_TILE], in_=acc[:])
+                acc = psum.tile([P, N_TILE], F32, tag="acc")
+                nc.tensor.matmul(out=acc[:], lhsT=row_selector(j), rhs=vector_rows[:, cols], start=True, stop=True)
+                copy(out=dst[:, cols], in_=acc[:])
 
-        bo_all = spread[:, 0:D]
-        gamma_all = spread[:, D : 2 * D]
-        beta_all = spread[:, 2 * D : 3 * D]
-        b1_all = spread[:, 3 * D : 5 * D]
+        o_all = keep.tile([P, TOKEN_TILES, D], BF16)
+        x_all = keep.tile([P, TOKEN_TILES, D], BF16)
+        wo_raw = keep.tile([P, PASSES, PACK, D], BF16)
+        w1_raw = keep.tile([P, PASSES, PACK, F], BF16)
+
+        def load_tokens(j):
+            nc.sync.dma_start(out=o_all[:, j, :], in_=o_tiles[j])
+            nc.sync.dma_start(out=x_all[:, j, :], in_=x_tiles[j])
+
+        def load_wo():
+            for g in range(PASSES):
+                for u in range(2):
+                    k0 = g * K_PASS + u * 2 * P
+                    nc.sync.dma_start(
+                        out=wo_raw[:, g, 2 * u : 2 * u + 2, :],
+                        in_=Wo[k0 : k0 + 2 * P, :].rearrange("(q e) c -> q e c", e=2),
+                    )
+
+        def load_w1(first):
+            cols = slice(first, first + HALF)
+            for g in range(PASSES):
+                nc.sync.dma_start(
+                    out=w1_raw[:, g, :, cols],
+                    in_=W1[g * K_PASS : (g + 1) * K_PASS, cols].rearrange("(t p) n -> p t n", p=P),
+                )
+
+        load_wo()
+        load_tokens(0)
+        load_tokens(1)
+        load_tokens(2)
+        load_w1(0)
+        load_tokens(3)
+        load_w1(HALF)
+        for j in range(4, TOKEN_TILES):
+            load_tokens(j)
 
         wo_codes = keep.tile([P, PASSES, D], U32, align_bytes=64)
         wo_scales = keep.tile([P, PASSES, D], U8, align_bytes=64)
         w1_codes = keep.tile([P, PASSES, F], U32, align_bytes=64)
         w1_scales = keep.tile([P, PASSES, F], U8, align_bytes=64)
 
-        def quantise_weights(copy, raw, codes, scales, g, n):
-            cols = slice(n * N_TILE, (n + 1) * N_TILE)
-            grouped = work.tile([P, N_TILE * PACK], BF16, align_bytes=64, tag="w_grouped", bufs=3)
-            copy(
-                out=grouped[:].rearrange("p (c i t) -> p c t i", i=4, t=PACK),
-                in_=raw[:, g, :, cols].rearrange("p t (c i) -> p c t i", i=4),
-            )
-            nc.vector.quantize_mx(
-                out=codes[:, g, cols].bitcast(FP8X4), scales=scales[:, g, cols], in_=grouped[:]
-            )
+        def regroup_weights(raw, first):
+            pieces = []
+            for g in range(PASSES):
+                for copy, start in ((nc.vector.tensor_copy, first), (nc.scalar.copy, first + N_TILE)):
+                    cols = slice(start, start + N_TILE)
+                    grouped = work.tile([P, N_TILE * PACK], BF16, align_bytes=64, tag="w_grouped", bufs=4)
+                    copy(
+                        out=grouped[:].rearrange("p (c i t) -> p c t i", i=4, t=PACK),
+                        in_=raw[:, g, :, cols].rearrange("p t (c i) -> p c t i", i=4),
+                    )
+                    pieces.append((grouped, g, cols))
+            return pieces
 
-        def copy_engine(chunk):
-            return nc.vector.tensor_copy if chunk % 2 == 0 else nc.scalar.copy
+        def quantise_weights(pieces, codes, scales):
+            for grouped, g, cols in pieces:
+                nc.vector.quantize_mx(
+                    out=codes[:, g, cols].bitcast(FP8X4), scales=scales[:, g, cols], in_=grouped[:]
+                )
 
-        biased = {}
-        heads = {}
-        normed = {}
+        def mx_group(acc, codes, scales, w_codes, w_scales, cols):
+            for g in range(PASSES):
+                toks = slice(g * P, (g + 1) * P)
+                nc.tensor.matmul_mx(
+                    out=acc[:],
+                    lhsT=codes[:, toks].bitcast(FP8X4),
+                    lhsT_scale=scales[:, toks],
+                    rhs=w_codes[:, g, cols].bitcast(FP8X4),
+                    rhs_scale=w_scales[:, g, cols],
+                    start=(g == 0),
+                    stop=(g == PASSES - 1),
+                )
 
-        def add_bias(i):
-            xb = work.tile([P, D], F32, tag="xb", bufs=3)
-            nc.vector.tensor_tensor(out=xb[:], in0=x_all[:, i, :], in1=bo_all, op=ALU.add)
-            biased[i] = xb
+        live = {}
 
-        def quantise_heads(i):
-            words = o_all[:, i, :].bitcast(F32)
-            flipped = psum.tile([P, PASSES * 2, P], F32, tag="flipped", bufs=2)
+        def flip_heads(j):
+            words = o_all[:, j, :].bitcast(F32)
+            flipped = psum.tile([P, PASSES * 2, P], F32, tag="flipped")
             for a in range(PASSES * 2):
                 nc.tensor.transpose(flipped[:, a, :], words[:, a * P : (a + 1) * P], ident_f32[:])
-            grouped = work.tile([P, D], BF16, align_bytes=64, tag="o_grouped", bufs=2)
+            live["o_flipped", j] = flipped
+
+        def copy_heads(j):
+            flipped = live.pop(("o_flipped", j))
+            grouped = work.tile([P, D], BF16, align_bytes=64, tag="o_grouped")
             nc.scalar.copy(
                 out=grouped[:].bitcast(F32).rearrange("p (g r u) -> p g r u", g=PASSES, u=2),
                 in_=flipped[:].rearrange("p (g u) r -> p g r u", u=2),
             )
-            codes = work.tile([P, PASSES * P], U32, align_bytes=64, tag="o_codes", bufs=3)
-            scales = work.tile([P, PASSES * P], U8, align_bytes=64, tag="o_scales", bufs=3)
-            nc.vector.quantize_mx(out=codes[:].bitcast(FP8X4), scales=scales[:], in_=grouped[:])
-            heads[i] = (codes, scales)
+            live["o_grouped", j] = grouped
 
-        def project_and_norm(i):
-            codes, scales = heads.pop(i)
-            xb = biased.pop(i)
-            residual = work.tile([P, D], F32, tag="residual", bufs=2)
-            row_sums = work.tile([P, D // N_TILE], F32, tag="row_sums", bufs=3)
+        def quantise_heads(j):
+            grouped = live.pop(("o_grouped", j))
+            codes = work.tile([P, PASSES * P], U32, align_bytes=64, tag="o_codes")
+            scales = work.tile([P, PASSES * P], U8, align_bytes=64, tag="o_scales")
+            nc.vector.quantize_mx(out=codes[:].bitcast(FP8X4), scales=scales[:], in_=grouped[:])
+            live["o_mx", j] = (codes, scales)
+
+        def bias_residual(j):
+            sums = []
             for n in range(D // N_TILE):
                 cols = slice(n * N_TILE, (n + 1) * N_TILE)
-                acc = psum.tile([P, N_TILE], F32, tag="acc1", bufs=2)
-                for g in range(PASSES):
-                    toks = slice(g * P, (g + 1) * P)
-                    nc.tensor.matmul_mx(
-                        out=acc[:],
-                        lhsT=codes[:, toks].bitcast(FP8X4),
-                        lhsT_scale=scales[:, toks],
-                        rhs=wo_codes[:, g, cols].bitcast(FP8X4),
-                        rhs_scale=wo_scales[:, g, cols],
-                        start=(g == 0),
-                        stop=(g == PASSES - 1),
-                    )
+                xb_sum = psum.tile([P, N_TILE], F32, tag="flipped")
+                nc.tensor.matmul(out=xb_sum[:], lhsT=ident_bf16[:], rhs=x_all[:, j, cols], start=True, stop=False)
+                nc.tensor.matmul(out=xb_sum[:], lhsT=row_selector(0), rhs=vector_rows[:, cols], start=False, stop=True)
+                sums.append(xb_sum)
+            live["xb_sums", j] = sums
+
+        def copy_biased(j):
+            xb = work.tile([P, D], F32, tag="xb")
+            for n, xb_sum in enumerate(live.pop(("xb_sums", j))):
+                nc.scalar.copy(out=xb[:, n * N_TILE : (n + 1) * N_TILE], in_=xb_sum[:])
+            live["xb", j] = xb
+
+        def project(j):
+            codes, scales = live.pop(("o_mx", j))
+            sums = []
+            for n in range(D // N_TILE):
+                acc = psum.tile([P, N_TILE], F32, tag="acc")
+                mx_group(acc, codes, scales, wo_codes, wo_scales, slice(n * N_TILE, (n + 1) * N_TILE))
+                sums.append(acc)
+            live["attn", j] = sums
+
+        def add_residual(j):
+            xb = live.pop(("xb", j))
+            residual = work.tile([P, D], F32, tag="residual")
+            row_sums = work.tile([P, D // N_TILE], F32, tag="row_sums")
+            for n, acc in enumerate(live.pop(("attn", j))):
+                cols = slice(n * N_TILE, (n + 1) * N_TILE)
                 nc.vector.scalar_tensor_tensor(
-                    out=residual[:, cols],
-                    in0=acc[:],
-                    scalar=1.0,
-                    in1=xb[:, cols],
-                    op0=ALU.mult,
-                    op1=ALU.add,
-                    accum_out=row_sums[:, n : n + 1],
+                    out=residual[:, cols], in0=acc[:], scalar=1.0, in1=xb[:, cols],
+                    op0=ALU.mult, op1=ALU.add, accum_out=row_sums[:, n : n + 1],
                 )
-            neg_mean = work.tile([P, 1], F32, tag="neg_mean", bufs=3)
+            live["residual", j] = residual
+            live["row_sums", j] = row_sums
+
+        def mean(j):
+            row_sums = live.pop(("row_sums", j))
+            neg_mean = work.tile([P, 1], F32, tag="neg_mean")
             nc.vector.tensor_scalar(
-                out=neg_mean[:],
-                in0=row_sums[:, 0:1],
-                scalar1=row_sums[:, 1:2],
-                scalar2=-1.0 / D,
-                op0=ALU.add,
-                op1=ALU.mult,
-            )
-            squares = work.tile([P, D], BF16, tag="squares", bufs=2)
-            sum_sq = work.tile([P, 1], F32, tag="sum_sq", bufs=3)
-            nc.scalar.activation(
-                out=squares[:], in_=residual[:], func=ACT.Square, bias=neg_mean[:], scale=1.0,
-                accum_out=sum_sq[:],
-            )
-            centred = work.tile([P, D], F32, tag="centred", bufs=2)
-            nc.vector.scalar_tensor_tensor(
-                out=centred[:], in0=residual[:], scalar=neg_mean[:], in1=gamma_all,
+                out=neg_mean[:], in0=row_sums[:, 0:1], scalar1=row_sums[:, 1:2], scalar2=-1.0 / D,
                 op0=ALU.add, op1=ALU.mult,
             )
-            var_eps = work.tile([P, 1], F32, tag="var_eps", bufs=3)
-            nc.gpsimd.tensor_scalar(
-                out=var_eps[:], in0=sum_sq[:], scalar1=1.0 / D, scalar2=EPS, op0=ALU.mult, op1=ALU.add
+            live["neg_mean", j] = neg_mean
+
+        def sum_squares(j):
+            squares = work.tile([P, D], BF16, tag="squares")
+            sum_sq = work.tile([P, 1], F32, tag="sum_sq")
+            nc.scalar.activation(
+                out=squares[:], in_=live["residual", j][:], func=ACT.Square,
+                bias=live["neg_mean", j][:], scale=1.0, accum_out=sum_sq[:],
             )
-            rstd = work.tile([P, 1], F32, tag="rstd", bufs=3)
+            live["sum_sq", j] = sum_sq
+
+        def centre(j):
+            centred = work.tile([P, D], F32, tag="centred")
+            nc.vector.scalar_tensor_tensor(
+                out=centred[:], in0=live.pop(("residual", j))[:], scalar=live.pop(("neg_mean", j))[:],
+                in1=gamma_all[:], op0=ALU.add, op1=ALU.mult,
+            )
+            live["centred", j] = centred
+
+        def inverse_std(j):
+            var_eps = work.tile([P, 1], F32, tag="var_eps")
+            nc.gpsimd.tensor_scalar(
+                out=var_eps[:], in0=live.pop(("sum_sq", j))[:], scalar1=1.0 / D, scalar2=EPS,
+                op0=ALU.mult, op1=ALU.add,
+            )
+            rstd = work.tile([P, 1], F32, tag="rstd")
             nc.gpsimd.tensor_tensor(out=rstd[:], in0=var_eps[:], in1=neg_half[:], op=ALU.pow)
+            live["rstd", j] = rstd
+
+        def normalise(j):
             xn = work.tile([P, D], F32, tag="xn", bufs=3)
             nc.vector.scalar_tensor_tensor(
-                out=xn[:], in0=centred[:], scalar=rstd[:], in1=beta_all, op0=ALU.mult, op1=ALU.add
+                out=xn[:], in0=live.pop(("centred", j))[:], scalar=live.pop(("rstd", j))[:],
+                in1=beta_all[:], op0=ALU.mult, op1=ALU.add,
             )
-            nc.sync.dma_start(out=xn_rows[:, i, :], in_=xn[:])
+            nc.sync.dma_start(out=xn_tiles[j], in_=xn[:])
+            live["xn", j] = xn
 
-            grouped = work.tile([P, D], BF16, align_bytes=64, tag="xn_grouped", bufs=2)
+        def flip_normed(j):
+            xn = live.pop(("xn", j))
+            grouped = work.tile([P, D], BF16, align_bytes=64, tag="xn_grouped")
             for g in range(PASSES):
-                flipped = psum.tile([P, PACK, P], F32, tag="flipped", bufs=2)
+                flipped = psum.tile([P, PACK, P], F32, tag="flipped")
                 for t in range(PACK):
                     k0 = g * K_PASS + t * P
                     nc.tensor.transpose(flipped[:, t, :], xn[:, k0 : k0 + P], ident_f32[:])
@@ -213,61 +263,81 @@ def tile_swablock_pb_kernel(tc, x, o_heads, Wo, bo, gamma, beta, W1, b1, out_0, 
                     out=grouped[:, g * K_PASS : (g + 1) * K_PASS].rearrange("p (r t) -> p r t", t=PACK),
                     in_=flipped[:].rearrange("p t r -> p r t"),
                 )
-            xn_codes = work.tile([P, PASSES * P], U32, align_bytes=64, tag="xn_codes", bufs=LAG + 2)
-            xn_scales = work.tile([P, PASSES * P], U8, align_bytes=64, tag="xn_scales", bufs=LAG + 2)
-            nc.vector.quantize_mx(out=xn_codes[:].bitcast(FP8X4), scales=xn_scales[:], in_=grouped[:])
-            normed[i] = (xn_codes, xn_scales)
+            live["xn_grouped", j] = grouped
 
-        def hidden_layer(i):
-            codes, scales = normed.pop(i)
-            for half in range(F // HALF):
-                hidden = work.tile([P, HALF], F32, tag="hidden", bufs=4)
-                for n in range(HALF // N_TILE):
-                    cols = slice(half * HALF + n * N_TILE, half * HALF + (n + 1) * N_TILE)
-                    acc = psum.tile([P, N_TILE], F32, tag="acc2", bufs=4)
-                    for g in range(PASSES):
-                        toks = slice(g * P, (g + 1) * P)
-                        nc.tensor.matmul_mx(
-                            out=acc[:],
-                            lhsT=codes[:, toks].bitcast(FP8X4),
-                            lhsT_scale=scales[:, toks],
-                            rhs=w1_codes[:, g, cols].bitcast(FP8X4),
-                            rhs_scale=w1_scales[:, g, cols],
-                            start=(g == 0),
-                            stop=(g == PASSES - 1),
-                        )
-                    nc.vector.tensor_tensor(
-                        out=hidden[:, n * N_TILE : (n + 1) * N_TILE], in0=acc[:], in1=b1_all[:, cols],
-                        op=ALU.add,
-                    )
-                nc.scalar.activation(out=hidden[:], in_=hidden[:], func=ACT.Gelu)
-                nc.sync.dma_start(out=h_rows[:, i, half * HALF : (half + 1) * HALF], in_=hidden[:])
+        def quantise_normed(j):
+            grouped = live.pop(("xn_grouped", j))
+            codes = work.tile([P, PASSES * P], U32, align_bytes=64, tag="xn_codes", bufs=LAG + 1)
+            scales = work.tile([P, PASSES * P], U8, align_bytes=64, tag="xn_scales", bufs=LAG + 1)
+            nc.vector.quantize_mx(out=codes[:].bitcast(FP8X4), scales=scales[:], in_=grouped[:])
+            live["xn_mx", j] = (codes, scales)
 
-        spread_row(0)
+        def hidden_matmuls(j):
+            codes, scales = live.pop(("xn_mx", j))
+            sums = []
+            for n in range(F // N_TILE):
+                acc = psum.tile([P, N_TILE], F32, tag="acc")
+                mx_group(acc, codes, scales, w1_codes, w1_scales, slice(n * N_TILE, (n + 1) * N_TILE))
+                sums.append(acc)
+            live["hidden_sums", j] = sums
+
+        def add_hidden_bias(j, first):
+            hidden = work.tile([P, HALF], F32, tag="hidden", bufs=4)
+            for n in range(HALF // N_TILE):
+                start = first + n * N_TILE
+                nc.vector.tensor_tensor(
+                    out=hidden[:, n * N_TILE : (n + 1) * N_TILE],
+                    in0=live["hidden_sums", j][start // N_TILE][:],
+                    in1=b1_all[:, start : start + N_TILE],
+                    op=ALU.add,
+                )
+            live["hidden", j, first] = hidden
+
+        def gelu_store(j, first):
+            hidden = live.pop(("hidden", j, first))
+            nc.scalar.activation(out=hidden[:], in_=hidden[:], func=ACT.Gelu)
+            nc.sync.dma_start(out=h_tiles[j][:, first : first + HALF], in_=hidden[:])
+
+        def in_range(stage, j, *args):
+            if 0 <= j < TOKEN_TILES:
+                stage(j, *args)
+
+        spread_row(1, nc.vector.tensor_copy, gamma_all)
+        spread_row(2, nc.vector.tensor_copy, beta_all)
+        quantise_weights(regroup_weights(wo_raw, 0), wo_codes, wo_scales)
+        flip_heads(0)
+        copy_heads(0)
         quantise_heads(0)
-        add_bias(0)
-        chunk = 0
-        for n in range(D // N_TILE):
-            for g in range(PASSES):
-                quantise_weights(copy_engine(chunk), wo_raw, wo_codes, wo_scales, g, n)
-                chunk += 1
-        spread_row(1)
-        spread_row(2)
+        bias_residual(0)
+        copy_biased(0)
+        flip_heads(1)
+        copy_heads(1)
+        project(0)
+        flip_heads(2)
+        bias_residual(1)
 
-        w1_chunks = [(g, n) for n in range(F // N_TILE) for g in range(PASSES)]
-        per_step = len(w1_chunks) // LAG
-        for step in range(TOKEN_TILES + LAG):
-            if step + 1 < TOKEN_TILES:
-                quantise_heads(step + 1)
-                add_bias(step + 1)
-            if step < TOKEN_TILES:
-                project_and_norm(step)
-            if step < LAG:
-                for g, n in w1_chunks[step * per_step : (step + 1) * per_step]:
-                    quantise_weights(copy_engine(chunk), w1_raw, w1_codes, w1_scales, g, n)
-                    chunk += 1
-            if step == 0:
-                spread_row(3)
-                spread_row(4)
-            if step >= LAG:
-                hidden_layer(step - LAG)
+        for i in range(TOKEN_TILES + LAG + 1):
+            in_range(gelu_store, i - LAG - 1, HALF)
+            in_range(add_residual, i)
+            in_range(quantise_heads, i + 1)
+            in_range(mean, i)
+            in_range(sum_squares, i)
+            in_range(quantise_normed, i - 1)
+            in_range(hidden_matmuls, i - LAG)
+            in_range(centre, i)
+            if i < LAG:
+                w1_pieces = regroup_weights(w1_raw, i * HALF)
+                spread_row(3 + i, nc.scalar.copy, b1_all[:, i * HALF : (i + 1) * HALF])
+            in_range(copy_heads, i + 2)
+            in_range(copy_biased, i + 1)
+            in_range(add_hidden_bias, i - LAG, 0)
+            in_range(project, i + 1)
+            in_range(gelu_store, i - LAG, 0)
+            in_range(inverse_std, i)
+            in_range(normalise, i)
+            in_range(flip_normed, i)
+            in_range(flip_heads, i + 3)
+            in_range(bias_residual, i + 2)
+            if i < LAG:
+                quantise_weights(w1_pieces, w1_codes, w1_scales)
+            in_range(add_hidden_bias, i - LAG, HALF)

@@ -111,11 +111,13 @@ def tile_swablock_pb_kernel(tc, x, o_heads, Wo, bo, gamma, beta, W1, b1, out_0, 
         w1_codes = keep.tile([P, PASSES, F], U32, align_bytes=64)
         w1_scales = keep.tile([P, PASSES, F], U8, align_bytes=64)
 
-        def regroup_weights(raw, first):
+        def regroup_weights(raw, first, scalar_pieces):
             pieces = []
             for g in range(PASSES):
-                for copy, start in ((nc.vector.tensor_copy, first), (nc.scalar.copy, first + N_TILE)):
-                    cols = slice(start, start + N_TILE)
+                for n in range(HALF // N_TILE):
+                    by_scalar = n == 1 and g >= PASSES - scalar_pieces
+                    copy = nc.scalar.copy if by_scalar else nc.vector.tensor_copy
+                    cols = slice(first + n * N_TILE, first + (n + 1) * N_TILE)
                     grouped = work.tile([P, N_TILE * PACK], BF16, align_bytes=64, tag="w_grouped", bufs=4)
                     copy(
                         out=grouped[:].rearrange("p (c i t) -> p c t i", i=4, t=PACK),
@@ -272,24 +274,23 @@ def tile_swablock_pb_kernel(tc, x, o_heads, Wo, bo, gamma, beta, W1, b1, out_0, 
             nc.vector.quantize_mx(out=codes[:].bitcast(FP8X4), scales=scales[:], in_=grouped[:])
             live["xn_mx", j] = (codes, scales)
 
-        def hidden_matmuls(j):
-            codes, scales = live.pop(("xn_mx", j))
+        def hidden_matmuls(j, first):
+            codes, scales = live["xn_mx", j] if first == 0 else live.pop(("xn_mx", j))
             sums = []
-            for n in range(F // N_TILE):
+            for n in range(HALF // N_TILE):
                 acc = psum.tile([P, N_TILE], F32, tag="acc")
-                mx_group(acc, codes, scales, w1_codes, w1_scales, slice(n * N_TILE, (n + 1) * N_TILE))
+                start = first + n * N_TILE
+                mx_group(acc, codes, scales, w1_codes, w1_scales, slice(start, start + N_TILE))
                 sums.append(acc)
-            live["hidden_sums", j] = sums
+            live["hidden_sums", j, first] = sums
 
         def add_hidden_bias(j, first):
             hidden = work.tile([P, HALF], F32, tag="hidden", bufs=4)
-            for n in range(HALF // N_TILE):
+            for n, acc in enumerate(live.pop(("hidden_sums", j, first))):
                 start = first + n * N_TILE
                 nc.vector.tensor_tensor(
-                    out=hidden[:, n * N_TILE : (n + 1) * N_TILE],
-                    in0=live["hidden_sums", j][start // N_TILE][:],
-                    in1=b1_all[:, start : start + N_TILE],
-                    op=ALU.add,
+                    out=hidden[:, n * N_TILE : (n + 1) * N_TILE], in0=acc[:],
+                    in1=b1_all[:, start : start + N_TILE], op=ALU.add,
                 )
             live["hidden", j, first] = hidden
 
@@ -304,7 +305,7 @@ def tile_swablock_pb_kernel(tc, x, o_heads, Wo, bo, gamma, beta, W1, b1, out_0, 
 
         spread_row(1, nc.vector.tensor_copy, gamma_all)
         spread_row(2, nc.vector.tensor_copy, beta_all)
-        quantise_weights(regroup_weights(wo_raw, 0), wo_codes, wo_scales)
+        quantise_weights(regroup_weights(wo_raw, 0, 2), wo_codes, wo_scales)
         flip_heads(0)
         copy_heads(0)
         quantise_heads(0)
@@ -312,32 +313,37 @@ def tile_swablock_pb_kernel(tc, x, o_heads, Wo, bo, gamma, beta, W1, b1, out_0, 
         copy_biased(0)
         flip_heads(1)
         copy_heads(1)
-        project(0)
-        flip_heads(2)
         bias_residual(1)
+        copy_biased(1)
+        flip_heads(2)
+        copy_heads(2)
+        bias_residual(2)
+        project(0)
 
-        for i in range(TOKEN_TILES + LAG + 1):
-            in_range(gelu_store, i - LAG - 1, HALF)
+        for i in range(TOKEN_TILES + LAG):
             in_range(add_residual, i)
+            in_range(hidden_matmuls, i - LAG, HALF)
+            if i < LAG:
+                spread_row(3 + i, nc.scalar.copy, b1_all[:, i * HALF : (i + 1) * HALF])
             in_range(quantise_heads, i + 1)
             in_range(mean, i)
             in_range(sum_squares, i)
-            in_range(quantise_normed, i - 1)
-            in_range(hidden_matmuls, i - LAG)
+            in_range(inverse_std, i)
+            in_range(normalise, i - 1)
+            in_range(copy_biased, i + 2)
+            in_range(flip_normed, i - 1)
+            in_range(flip_heads, i + 3)
+            in_range(add_hidden_bias, i - LAG, 0)
+            in_range(gelu_store, i - LAG, 0)
+            in_range(project, i + 1)
+            in_range(bias_residual, i + 3)
             in_range(centre, i)
             if i < LAG:
-                w1_pieces = regroup_weights(w1_raw, i * HALF)
-                spread_row(3 + i, nc.scalar.copy, b1_all[:, i * HALF : (i + 1) * HALF])
-            in_range(copy_heads, i + 2)
-            in_range(copy_biased, i + 1)
-            in_range(add_hidden_bias, i - LAG, 0)
-            in_range(project, i + 1)
-            in_range(gelu_store, i - LAG, 0)
-            in_range(inverse_std, i)
-            in_range(normalise, i)
-            in_range(flip_normed, i)
-            in_range(flip_heads, i + 3)
-            in_range(bias_residual, i + 2)
+                w1_pieces = regroup_weights(w1_raw, i * HALF, 1)
+            in_range(add_hidden_bias, i - LAG, HALF)
+            in_range(gelu_store, i - LAG, HALF)
+            in_range(copy_heads, i + 3)
+            in_range(quantise_normed, i - 1)
             if i < LAG:
                 quantise_weights(w1_pieces, w1_codes, w1_scales)
-            in_range(add_hidden_bias, i - LAG, HALF)
+            in_range(hidden_matmuls, i - LAG + 1, 0)

@@ -48,7 +48,7 @@ def tile_swablock_pb_kernel(tc, x, o_heads, Wo, bo, gamma, beta, W1, b1, out_0, 
         nc.vector.memset(neg_half[:], -0.5)
 
         vector_rows = keep.tile([P, D], BF16)
-        nc.vector.memset(vector_rows[:], 0.0)
+        nc.vector.memset(vector_rows[:].bitcast(U32), 0)
         nc.scalar.dma_start(out=vector_rows[0:1, :], in_=bo.unsqueeze(0))
         nc.scalar.dma_start(out=vector_rows[1:2, :], in_=gamma.unsqueeze(0))
         nc.scalar.dma_start(out=vector_rows[2:3, :], in_=beta.unsqueeze(0))
@@ -81,12 +81,14 @@ def tile_swablock_pb_kernel(tc, x, o_heads, Wo, bo, gamma, beta, W1, b1, out_0, 
 
         def load_wo():
             for g in range(PASSES):
-                for u in range(2):
-                    k0 = g * K_PASS + u * 2 * P
-                    nc.sync.dma_start(
-                        out=wo_raw[:, g, 2 * u : 2 * u + 2, :],
-                        in_=Wo[k0 : k0 + 2 * P, :].rearrange("(q e) c -> q e c", e=2),
-                    )
+                for n in range(D // N_TILE):
+                    cols = slice(n * N_TILE, (n + 1) * N_TILE)
+                    for u in range(2):
+                        k0 = g * K_PASS + u * 2 * P
+                        nc.sync.dma_start(
+                            out=wo_raw[:, g, 2 * u : 2 * u + 2, cols],
+                            in_=Wo[k0 : k0 + 2 * P, cols].rearrange("(q e) c -> q e c", e=2),
+                        )
 
         def load_w1(first):
             cols = slice(first, first + HALF)
@@ -96,8 +98,9 @@ def tile_swablock_pb_kernel(tc, x, o_heads, Wo, bo, gamma, beta, W1, b1, out_0, 
                     in_=W1[g * K_PASS : (g + 1) * K_PASS, cols].rearrange("(t p) n -> p t n", p=P),
                 )
 
+        nc.sync.dma_start(out=o_all[:, 0, :], in_=o_tiles[0])
         load_wo()
-        load_tokens(0)
+        nc.sync.dma_start(out=x_all[:, 0, :], in_=x_tiles[0])
         load_tokens(1)
         load_tokens(2)
         load_w1(0)
@@ -294,33 +297,36 @@ def tile_swablock_pb_kernel(tc, x, o_heads, Wo, bo, gamma, beta, W1, b1, out_0, 
                 )
             live["hidden", j, first] = hidden
 
-        def gelu_store(j, first):
+        def gelu_store(j, first, width=HALF):
             hidden = live.pop(("hidden", j, first))
-            nc.scalar.activation(out=hidden[:], in_=hidden[:], func=ACT.Gelu)
-            nc.sync.dma_start(out=h_tiles[j][:, first : first + HALF], in_=hidden[:])
+            for c in range(0, HALF, width):
+                piece = hidden[:, c : c + width]
+                nc.scalar.activation(out=piece, in_=piece, func=ACT.Gelu)
+                nc.sync.dma_start(out=h_tiles[j][:, first + c : first + c + width], in_=piece)
 
         def in_range(stage, j, *args):
             if 0 <= j < TOKEN_TILES:
                 stage(j, *args)
 
-        spread_row(1, nc.vector.tensor_copy, gamma_all)
-        spread_row(2, nc.vector.tensor_copy, beta_all)
-        quantise_weights(regroup_weights(wo_raw, 0, 2), wo_codes, wo_scales)
         flip_heads(0)
         copy_heads(0)
+        wo_pieces = regroup_weights(wo_raw, 0, 1)
+        spread_row(1, nc.scalar.copy, gamma_all)
         quantise_heads(0)
+        quantise_weights(wo_pieces, wo_codes, wo_scales)
         bias_residual(0)
         copy_biased(0)
         flip_heads(1)
         copy_heads(1)
+        project(0)
         bias_residual(1)
         copy_biased(1)
         flip_heads(2)
         copy_heads(2)
+        spread_row(2, nc.scalar.copy, beta_all)
         bias_residual(2)
-        project(0)
 
-        for i in range(TOKEN_TILES + LAG):
+        for i in range(TOKEN_TILES - 1):
             in_range(add_residual, i)
             in_range(hidden_matmuls, i - LAG, HALF)
             if i < LAG:
@@ -339,7 +345,7 @@ def tile_swablock_pb_kernel(tc, x, o_heads, Wo, bo, gamma, beta, W1, b1, out_0, 
             in_range(bias_residual, i + 3)
             in_range(centre, i)
             if i < LAG:
-                w1_pieces = regroup_weights(w1_raw, i * HALF, 1)
+                w1_pieces = regroup_weights(w1_raw, i * HALF, 1 + i)
             in_range(add_hidden_bias, i - LAG, HALF)
             in_range(gelu_store, i - LAG, HALF)
             in_range(copy_heads, i + 3)
@@ -347,3 +353,33 @@ def tile_swablock_pb_kernel(tc, x, o_heads, Wo, bo, gamma, beta, W1, b1, out_0, 
             if i < LAG:
                 quantise_weights(w1_pieces, w1_codes, w1_scales)
             in_range(hidden_matmuls, i - LAG + 1, 0)
+
+        j = TOKEN_TILES - 1
+        add_residual(j)
+        hidden_matmuls(j - 2, HALF)
+        mean(j)
+        sum_squares(j)
+        inverse_std(j)
+        normalise(j - 1)
+        flip_normed(j - 1)
+        add_hidden_bias(j - 2, 0)
+        gelu_store(j - 2, 0)
+        centre(j)
+        normalise(j)
+        flip_normed(j)
+        quantise_normed(j - 1)
+        hidden_matmuls(j - 1, 0)
+        add_hidden_bias(j - 2, HALF)
+        gelu_store(j - 2, HALF)
+        add_hidden_bias(j - 1, 0)
+        gelu_store(j - 1, 0)
+        quantise_normed(j)
+        hidden_matmuls(j - 1, HALF)
+        hidden_matmuls(j, 0)
+        add_hidden_bias(j - 1, HALF)
+        gelu_store(j - 1, HALF)
+        hidden_matmuls(j, HALF)
+        add_hidden_bias(j, 0)
+        gelu_store(j, 0)
+        add_hidden_bias(j, HALF)
+        gelu_store(j, HALF, N_TILE)

@@ -82,6 +82,8 @@ def tile_swablock_pb_kernel(tc, x, o_heads, Wo, bo, gamma, beta, W1, b1, out_0, 
         def load_wo():
             for g in range(PASSES):
                 for n in range(D // N_TILE):
+                    if (g, n) == (0, 1):
+                        nc.sync.dma_start(out=o_all[:, 0, :], in_=o_tiles[0])
                     cols = slice(n * N_TILE, (n + 1) * N_TILE)
                     for u in range(2):
                         k0 = g * K_PASS + u * 2 * P
@@ -98,14 +100,15 @@ def tile_swablock_pb_kernel(tc, x, o_heads, Wo, bo, gamma, beta, W1, b1, out_0, 
                     in_=W1[g * K_PASS : (g + 1) * K_PASS, cols].rearrange("(t p) n -> p t n", p=P),
                 )
 
-        nc.sync.dma_start(out=o_all[:, 0, :], in_=o_tiles[0])
         load_wo()
         nc.sync.dma_start(out=x_all[:, 0, :], in_=x_tiles[0])
         load_tokens(1)
-        load_tokens(2)
+        nc.sync.dma_start(out=o_all[:, 2, :], in_=o_tiles[2])
         load_w1(0)
+        nc.sync.dma_start(out=x_all[:, 2, :], in_=x_tiles[2])
         load_tokens(3)
         load_w1(HALF)
+        nc.sync.dma_start(out=b1_all[:], in_=b1.partition_broadcast(P))
         for j in range(4, TOKEN_TILES):
             load_tokens(j)
 
@@ -114,26 +117,18 @@ def tile_swablock_pb_kernel(tc, x, o_heads, Wo, bo, gamma, beta, W1, b1, out_0, 
         w1_codes = keep.tile([P, PASSES, F], U32, align_bytes=64)
         w1_scales = keep.tile([P, PASSES, F], U8, align_bytes=64)
 
-        def regroup_weights(raw, first, scalar_pieces):
-            pieces = []
-            for g in range(PASSES):
-                for n in range(HALF // N_TILE):
-                    by_scalar = n == 1 and g >= PASSES - scalar_pieces
-                    copy = nc.scalar.copy if by_scalar else nc.vector.tensor_copy
-                    cols = slice(first + n * N_TILE, first + (n + 1) * N_TILE)
-                    grouped = work.tile([P, N_TILE * PACK], BF16, align_bytes=64, tag="w_grouped", bufs=4)
-                    copy(
-                        out=grouped[:].rearrange("p (c i t) -> p c t i", i=4, t=PACK),
-                        in_=raw[:, g, :, cols].rearrange("p t (c i) -> p c t i", i=4),
-                    )
-                    pieces.append((grouped, g, cols))
-            return pieces
+        def regroup(raw, g, n, copy):
+            cols = slice(n * N_TILE, (n + 1) * N_TILE)
+            grouped = work.tile([P, N_TILE * PACK], BF16, align_bytes=64, tag="w_grouped", bufs=4)
+            copy(
+                out=grouped[:].rearrange("p (c i t) -> p c t i", i=4, t=PACK),
+                in_=raw[:, g, :, cols].rearrange("p t (c i) -> p c t i", i=4),
+            )
+            return grouped, g, cols
 
-        def quantise_weights(pieces, codes, scales):
-            for grouped, g, cols in pieces:
-                nc.vector.quantize_mx(
-                    out=codes[:, g, cols].bitcast(FP8X4), scales=scales[:, g, cols], in_=grouped[:]
-                )
+        def quantise(piece, codes, scales):
+            grouped, g, cols = piece
+            nc.vector.quantize_mx(out=codes[:, g, cols].bitcast(FP8X4), scales=scales[:, g, cols], in_=grouped[:])
 
         def mx_group(acc, codes, scales, w_codes, w_scales, cols):
             for g in range(PASSES):
@@ -214,7 +209,7 @@ def tile_swablock_pb_kernel(tc, x, o_heads, Wo, bo, gamma, beta, W1, b1, out_0, 
         def mean(j):
             row_sums = live.pop(("row_sums", j))
             neg_mean = work.tile([P, 1], F32, tag="neg_mean")
-            nc.vector.tensor_scalar(
+            nc.gpsimd.tensor_scalar(
                 out=neg_mean[:], in0=row_sums[:, 0:1], scalar1=row_sums[:, 1:2], scalar2=-1.0 / D,
                 op0=ALU.add, op1=ALU.mult,
             )
@@ -288,7 +283,7 @@ def tile_swablock_pb_kernel(tc, x, o_heads, Wo, bo, gamma, beta, W1, b1, out_0, 
             live["hidden_sums", j, first] = sums
 
         def add_hidden_bias(j, first):
-            hidden = work.tile([P, HALF], F32, tag="hidden", bufs=4)
+            hidden = work.tile([P, HALF], F32, tag="hidden", bufs=6)
             for n, acc in enumerate(live.pop(("hidden_sums", j, first))):
                 start = first + n * N_TILE
                 nc.vector.tensor_tensor(
@@ -310,10 +305,15 @@ def tile_swablock_pb_kernel(tc, x, o_heads, Wo, bo, gamma, beta, W1, b1, out_0, 
 
         flip_heads(0)
         copy_heads(0)
-        wo_pieces = regroup_weights(wo_raw, 0, 1)
         spread_row(1, nc.scalar.copy, gamma_all)
+        spread_row(2, nc.scalar.copy, beta_all)
+        wo00 = regroup(wo_raw, 0, 0, nc.vector.tensor_copy)
+        wo01 = regroup(wo_raw, 0, 1, nc.vector.tensor_copy)
+        wo10 = regroup(wo_raw, 1, 0, nc.vector.tensor_copy)
+        wo11 = regroup(wo_raw, 1, 1, nc.scalar.copy)
         quantise_heads(0)
-        quantise_weights(wo_pieces, wo_codes, wo_scales)
+        for piece in (wo00, wo01, wo10, wo11):
+            quantise(piece, wo_codes, wo_scales)
         bias_residual(0)
         copy_biased(0)
         flip_heads(1)
@@ -323,14 +323,18 @@ def tile_swablock_pb_kernel(tc, x, o_heads, Wo, bo, gamma, beta, W1, b1, out_0, 
         copy_biased(1)
         flip_heads(2)
         copy_heads(2)
-        spread_row(2, nc.scalar.copy, beta_all)
         bias_residual(2)
 
+        PLAN_V = {0: [(0,0),(1,0),(0,1)], 1: [(0,2),(1,2)]}
+        PLAN_S = {0: [(1,1)], 1: [(0,3),(1,3)]}
+        PLAN_Q = {0: [(0,0),(1,0),(0,1)], 1: [(1,1),(0,2),(1,2),(0,3)]}
+        PLAN_Q0 = {2: [(1,3)]}
+        pieces = {}
         for i in range(TOKEN_TILES - 1):
             in_range(add_residual, i)
+            for name in PLAN_Q0.get(i, []):
+                quantise(pieces.pop(name), w1_codes, w1_scales)
             in_range(hidden_matmuls, i - LAG, HALF)
-            if i < LAG:
-                spread_row(3 + i, nc.scalar.copy, b1_all[:, i * HALF : (i + 1) * HALF])
             in_range(quantise_heads, i + 1)
             in_range(mean, i)
             in_range(sum_squares, i)
@@ -344,14 +348,16 @@ def tile_swablock_pb_kernel(tc, x, o_heads, Wo, bo, gamma, beta, W1, b1, out_0, 
             in_range(project, i + 1)
             in_range(bias_residual, i + 3)
             in_range(centre, i)
-            if i < LAG:
-                w1_pieces = regroup_weights(w1_raw, i * HALF, 1 + i)
+            for g, n in PLAN_V.get(i, []):
+                pieces[g, n] = regroup(w1_raw, g, n, nc.vector.tensor_copy)
             in_range(add_hidden_bias, i - LAG, HALF)
             in_range(gelu_store, i - LAG, HALF)
             in_range(copy_heads, i + 3)
+            for g, n in PLAN_S.get(i, []):
+                pieces[g, n] = regroup(w1_raw, g, n, nc.scalar.copy)
             in_range(quantise_normed, i - 1)
-            if i < LAG:
-                quantise_weights(w1_pieces, w1_codes, w1_scales)
+            for name in PLAN_Q.get(i, []):
+                quantise(pieces.pop(name), w1_codes, w1_scales)
             in_range(hidden_matmuls, i - LAG + 1, 0)
 
         j = TOKEN_TILES - 1
@@ -365,16 +371,16 @@ def tile_swablock_pb_kernel(tc, x, o_heads, Wo, bo, gamma, beta, W1, b1, out_0, 
         add_hidden_bias(j - 2, 0)
         gelu_store(j - 2, 0)
         centre(j)
-        normalise(j)
-        flip_normed(j)
         quantise_normed(j - 1)
         hidden_matmuls(j - 1, 0)
+        normalise(j)
+        flip_normed(j)
         add_hidden_bias(j - 2, HALF)
         gelu_store(j - 2, HALF)
+        hidden_matmuls(j - 1, HALF)
         add_hidden_bias(j - 1, 0)
         gelu_store(j - 1, 0)
         quantise_normed(j)
-        hidden_matmuls(j - 1, HALF)
         hidden_matmuls(j, 0)
         add_hidden_bias(j - 1, HALF)
         gelu_store(j - 1, HALF)

@@ -209,7 +209,7 @@ def tile_swablock_pb_kernel(tc, x, o_heads, Wo, bo, gamma, beta, W1, b1, out_0, 
         def mean(j):
             row_sums = live.pop(("row_sums", j))
             neg_mean = work.tile([P, 1], F32, tag="neg_mean")
-            nc.gpsimd.tensor_scalar(
+            nc.vector.tensor_scalar(
                 out=neg_mean[:], in0=row_sums[:, 0:1], scalar1=row_sums[:, 1:2], scalar2=-1.0 / D,
                 op0=ALU.add, op1=ALU.mult,
             )

@@ -72,8 +72,8 @@ def tile_swablock_pb_kernel(tc, x, o_heads, Wo, bo, gamma, beta, W1, b1, out_0, 
 
         o_all = keep.tile([P, TOKEN_TILES, D], BF16)
         x_all = keep.tile([P, TOKEN_TILES, D], BF16)
-        wo_raw = keep.tile([P, PASSES, PACK, D], BF16)
-        w1_raw = keep.tile([P, PASSES, PACK, F], BF16)
+        wo_raw = [keep.tile([P, PASSES, PACK, N_TILE], BF16, name="wo_raw%d" % n) for n in range(D // N_TILE)]
+        w1_raw = [keep.tile([P, PASSES, PACK, HALF], BF16, name="w1_raw%d" % n) for n in range(F // HALF)]
 
         def load_tokens(j):
             nc.sync.dma_start(out=o_all[:, j, :], in_=o_tiles[j])
@@ -88,7 +88,7 @@ def tile_swablock_pb_kernel(tc, x, o_heads, Wo, bo, gamma, beta, W1, b1, out_0, 
                     for u in range(2):
                         k0 = g * K_PASS + u * 2 * P
                         nc.sync.dma_start(
-                            out=wo_raw[:, g, 2 * u : 2 * u + 2, cols],
+                            out=wo_raw[n][:, g, 2 * u : 2 * u + 2, :],
                             in_=Wo[k0 : k0 + 2 * P, cols].rearrange("(q e) c -> q e c", e=2),
                         )
 
@@ -96,7 +96,7 @@ def tile_swablock_pb_kernel(tc, x, o_heads, Wo, bo, gamma, beta, W1, b1, out_0, 
             cols = slice(first, first + HALF)
             for g in range(PASSES):
                 nc.sync.dma_start(
-                    out=w1_raw[:, g, :, cols],
+                    out=w1_raw[first // HALF][:, g, :, :],
                     in_=W1[g * K_PASS : (g + 1) * K_PASS, cols].rearrange("(t p) n -> p t n", p=P),
                 )
 
@@ -117,12 +117,15 @@ def tile_swablock_pb_kernel(tc, x, o_heads, Wo, bo, gamma, beta, W1, b1, out_0, 
         w1_codes = keep.tile([P, PASSES, F], U32, align_bytes=64)
         w1_scales = keep.tile([P, PASSES, F], U8, align_bytes=64)
 
-        def regroup(raw, g, n, copy):
+        def regroup(raw_tiles, g, n, copy):
             cols = slice(n * N_TILE, (n + 1) * N_TILE)
+            tile_cols = raw_tiles[0].shape[3]
+            raw = raw_tiles[n * N_TILE // tile_cols]
+            first = n * N_TILE % tile_cols
             grouped = work.tile([P, N_TILE * PACK], BF16, align_bytes=64, tag="w_grouped", bufs=4)
             copy(
                 out=grouped[:].rearrange("p (c i t) -> p c t i", i=4, t=PACK),
-                in_=raw[:, g, :, cols].rearrange("p t (c i) -> p c t i", i=4),
+                in_=raw[:, g, :, first : first + N_TILE].rearrange("p t (c i) -> p c t i", i=4),
             )
             return grouped, g, cols
 

@@ -103,14 +103,14 @@ def tile_swablock_pb_kernel(tc, x, o_heads, Wo, bo, gamma, beta, W1, b1, out_0, 
         load_wo()
         nc.sync.dma_start(out=x_all[:, 0, :], in_=x_tiles[0])
         load_tokens(1)
-        nc.sync.dma_start(out=o_all[:, 2, :], in_=o_tiles[2])
+        load_tokens(2)
         load_w1(0)
-        nc.sync.dma_start(out=x_all[:, 2, :], in_=x_tiles[2])
         load_tokens(3)
         load_w1(HALF)
-        nc.sync.dma_start(out=b1_all[:], in_=b1.partition_broadcast(P))
         for j in range(4, TOKEN_TILES):
             load_tokens(j)
+            if j == 6:
+                nc.sync.dma_start(out=b1_all[:], in_=b1.partition_broadcast(P))
 
         wo_codes = keep.tile([P, PASSES, D], U32, align_bytes=64)
         wo_scales = keep.tile([P, PASSES, D], U8, align_bytes=64)
@@ -122,7 +122,7 @@ def tile_swablock_pb_kernel(tc, x, o_heads, Wo, bo, gamma, beta, W1, b1, out_0, 
             tile_cols = raw_tiles[0].shape[3]
             raw = raw_tiles[n * N_TILE // tile_cols]
             first = n * N_TILE % tile_cols
-            grouped = work.tile([P, N_TILE * PACK], BF16, align_bytes=64, tag="w_grouped", bufs=4)
+            grouped = work.tile([P, N_TILE * PACK], BF16, align_bytes=64, tag="w_grouped", bufs=5)
             copy(
                 out=grouped[:].rearrange("p (c i t) -> p c t i", i=4, t=PACK),
                 in_=raw[:, g, :, first : first + N_TILE].rearrange("p t (c i) -> p c t i", i=4),
@@ -210,16 +210,15 @@ def tile_swablock_pb_kernel(tc, x, o_heads, Wo, bo, gamma, beta, W1, b1, out_0, 
             live["row_sums", j] = row_sums
 
         def mean(j):
-            row_sums = live.pop(("row_sums", j))
+            parts = work.tile([P, D // N_TILE], F32, tag="mean_parts")
             neg_mean = work.tile([P, 1], F32, tag="neg_mean")
-            nc.vector.tensor_scalar(
-                out=neg_mean[:], in0=row_sums[:, 0:1], scalar1=row_sums[:, 1:2], scalar2=-1.0 / D,
-                op0=ALU.add, op1=ALU.mult,
+            nc.scalar.activation(
+                out=parts[:], in_=live.pop(("row_sums", j))[:], func=ACT.Copy, scale=-1.0 / D, accum_out=neg_mean[:]
             )
             live["neg_mean", j] = neg_mean
 
         def sum_squares(j):
-            squares = work.tile([P, D], BF16, tag="squares")
+            squares = work.tile([P, D], BF16, tag="squares", bufs=1)
             sum_sq = work.tile([P, 1], F32, tag="sum_sq")
             nc.scalar.activation(
                 out=squares[:], in_=live["residual", j][:], func=ACT.Square,
@@ -312,11 +311,13 @@ def tile_swablock_pb_kernel(tc, x, o_heads, Wo, bo, gamma, beta, W1, b1, out_0, 
         spread_row(2, nc.scalar.copy, beta_all)
         wo00 = regroup(wo_raw, 0, 0, nc.vector.tensor_copy)
         wo01 = regroup(wo_raw, 0, 1, nc.vector.tensor_copy)
+        quantise(wo00, wo_codes, wo_scales)
+        quantise(wo01, wo_codes, wo_scales)
         wo10 = regroup(wo_raw, 1, 0, nc.vector.tensor_copy)
         wo11 = regroup(wo_raw, 1, 1, nc.scalar.copy)
         quantise_heads(0)
-        for piece in (wo00, wo01, wo10, wo11):
-            quantise(piece, wo_codes, wo_scales)
+        quantise(wo10, wo_codes, wo_scales)
+        quantise(wo11, wo_codes, wo_scales)
         bias_residual(0)
         copy_biased(0)
         flip_heads(1)
@@ -328,9 +329,10 @@ def tile_swablock_pb_kernel(tc, x, o_heads, Wo, bo, gamma, beta, W1, b1, out_0, 
         copy_heads(2)
         bias_residual(2)
 
-        PLAN_V = {0: [(0,0),(1,0),(0,1)], 1: [(0,2),(1,2)]}
-        PLAN_S = {0: [(1,1)], 1: [(0,3),(1,3)]}
-        PLAN_Q = {0: [(0,0),(1,0),(0,1)], 1: [(1,1),(0,2),(1,2),(0,3)]}
+        PLAN_V = {0: [(0,0),(1,0)], 1: [(0,2),(1,2)]}
+        PLAN_S = {0: [(0,1),(1,1)], 1: [(0,3),(1,3)]}
+        PLAN_QA = {1: [(0,1),(1,1),(0,2),(1,2)]}
+        PLAN_Q = {0: [(0,0),(1,0)], 1: [(0,3)]}
         PLAN_Q0 = {2: [(1,3)]}
         pieces = {}
         for i in range(TOKEN_TILES - 1):
@@ -345,7 +347,8 @@ def tile_swablock_pb_kernel(tc, x, o_heads, Wo, bo, gamma, beta, W1, b1, out_0, 
             in_range(normalise, i - 1)
             in_range(copy_biased, i + 2)
             in_range(flip_normed, i - 1)
-            in_range(flip_heads, i + 3)
+            if i > 0:
+                in_range(flip_heads, i + 3)
             in_range(add_hidden_bias, i - LAG, 0)
             in_range(gelu_store, i - LAG, 0)
             in_range(project, i + 1)
@@ -355,9 +358,13 @@ def tile_swablock_pb_kernel(tc, x, o_heads, Wo, bo, gamma, beta, W1, b1, out_0, 
                 pieces[g, n] = regroup(w1_raw, g, n, nc.vector.tensor_copy)
             in_range(add_hidden_bias, i - LAG, HALF)
             in_range(gelu_store, i - LAG, HALF)
-            in_range(copy_heads, i + 3)
             for g, n in PLAN_S.get(i, []):
                 pieces[g, n] = regroup(w1_raw, g, n, nc.scalar.copy)
+            if i == 0:
+                flip_heads(3)
+            in_range(copy_heads, i + 3)
+            for name in PLAN_QA.get(i, []):
+                quantise(pieces.pop(name), w1_codes, w1_scales)
             in_range(quantise_normed, i - 1)
             for name in PLAN_Q.get(i, []):
                 quantise(pieces.pop(name), w1_codes, w1_scales)
@@ -371,13 +378,13 @@ def tile_swablock_pb_kernel(tc, x, o_heads, Wo, bo, gamma, beta, W1, b1, out_0, 
         inverse_std(j)
         normalise(j - 1)
         flip_normed(j - 1)
-        add_hidden_bias(j - 2, 0)
-        gelu_store(j - 2, 0)
         centre(j)
-        quantise_normed(j - 1)
-        hidden_matmuls(j - 1, 0)
         normalise(j)
         flip_normed(j)
+        add_hidden_bias(j - 2, 0)
+        gelu_store(j - 2, 0)
+        quantise_normed(j - 1)
+        hidden_matmuls(j - 1, 0)
         add_hidden_bias(j - 2, HALF)
         gelu_store(j - 2, HALF)
         hidden_matmuls(j - 1, HALF)

@@ -255,13 +255,18 @@ def tile_swablock_pb_kernel(tc, x, o_heads, Wo, bo, gamma, beta, W1, b1, out_0, 
 
         def flip_normed(j):
             xn = live.pop(("xn", j))
-            grouped = work.tile([P, D], BF16, align_bytes=64, tag="xn_grouped")
+            live["xn_flipped", j] = []
             for g in range(PASSES):
                 flipped = psum.tile([P, PACK, P], F32, tag="flipped")
                 for t in range(PACK):
                     k0 = g * K_PASS + t * P
                     nc.tensor.transpose(flipped[:, t, :], xn[:, k0 : k0 + P], ident_f32[:])
-                nc.scalar.copy(
+                live["xn_flipped", j].append(flipped)
+
+        def copy_normed(j, copies=(nc.scalar.copy, nc.scalar.copy)):
+            grouped = work.tile([P, D], BF16, align_bytes=64, tag="xn_grouped")
+            for g, flipped in enumerate(live.pop(("xn_flipped", j))):
+                copies[g](
                     out=grouped[:, g * K_PASS : (g + 1) * K_PASS].rearrange("p (r t) -> p r t", t=PACK),
                     in_=flipped[:].rearrange("p t r -> p r t"),
                 )
@@ -313,11 +318,11 @@ def tile_swablock_pb_kernel(tc, x, o_heads, Wo, bo, gamma, beta, W1, b1, out_0, 
         wo01 = regroup(wo_raw, 0, 1, nc.vector.tensor_copy)
         quantise(wo00, wo_codes, wo_scales)
         quantise(wo01, wo_codes, wo_scales)
-        wo10 = regroup(wo_raw, 1, 0, nc.vector.tensor_copy)
-        wo11 = regroup(wo_raw, 1, 1, nc.scalar.copy)
+        wo10 = regroup(wo_raw, 1, 0, nc.scalar.copy)
+        wo11 = regroup(wo_raw, 1, 1, nc.vector.tensor_copy)
         quantise_heads(0)
-        quantise(wo10, wo_codes, wo_scales)
         quantise(wo11, wo_codes, wo_scales)
+        quantise(wo10, wo_codes, wo_scales)
         bias_residual(0)
         copy_biased(0)
         flip_heads(1)
@@ -326,7 +331,6 @@ def tile_swablock_pb_kernel(tc, x, o_heads, Wo, bo, gamma, beta, W1, b1, out_0, 
         bias_residual(1)
         copy_biased(1)
         flip_heads(2)
-        copy_heads(2)
         bias_residual(2)
 
         PLAN_V = {0: [(0,0),(1,0)], 1: [(0,2),(1,2)]}
@@ -343,20 +347,23 @@ def tile_swablock_pb_kernel(tc, x, o_heads, Wo, bo, gamma, beta, W1, b1, out_0, 
             in_range(quantise_heads, i + 1)
             in_range(mean, i)
             in_range(sum_squares, i)
+            if i == 0:
+                copy_heads(2)
             in_range(inverse_std, i)
             in_range(normalise, i - 1)
             in_range(copy_biased, i + 2)
             in_range(flip_normed, i - 1)
+            in_range(copy_normed, i - 1)
             if i > 0:
                 in_range(flip_heads, i + 3)
             in_range(add_hidden_bias, i - LAG, 0)
             in_range(gelu_store, i - LAG, 0)
             in_range(project, i + 1)
             in_range(bias_residual, i + 3)
+            in_range(add_hidden_bias, i - LAG, HALF)
             in_range(centre, i)
             for g, n in PLAN_V.get(i, []):
                 pieces[g, n] = regroup(w1_raw, g, n, nc.vector.tensor_copy)
-            in_range(add_hidden_bias, i - LAG, HALF)
             in_range(gelu_store, i - LAG, HALF)
             for g, n in PLAN_S.get(i, []):
                 pieces[g, n] = regroup(w1_raw, g, n, nc.scalar.copy)
@@ -378,13 +385,15 @@ def tile_swablock_pb_kernel(tc, x, o_heads, Wo, bo, gamma, beta, W1, b1, out_0, 
         inverse_std(j)
         normalise(j - 1)
         flip_normed(j - 1)
+        copy_normed(j - 1)
         centre(j)
         normalise(j)
         flip_normed(j)
         add_hidden_bias(j - 2, 0)
-        gelu_store(j - 2, 0)
         quantise_normed(j - 1)
         hidden_matmuls(j - 1, 0)
+        copy_normed(j, (nc.scalar.copy, nc.vector.tensor_copy))
+        gelu_store(j - 2, 0)
         add_hidden_bias(j - 2, HALF)
         gelu_store(j - 2, HALF)
         hidden_matmuls(j - 1, HALF)
@@ -393,9 +402,9 @@ def tile_swablock_pb_kernel(tc, x, o_heads, Wo, bo, gamma, beta, W1, b1, out_0, 
         quantise_normed(j)
         hidden_matmuls(j, 0)
         add_hidden_bias(j - 1, HALF)
-        gelu_store(j - 1, HALF)
+        gelu_store(j - 1, HALF, N_TILE)
         hidden_matmuls(j, HALF)
         add_hidden_bias(j, 0)
-        gelu_store(j, 0)
+        gelu_store(j, 0, N_TILE)
         add_hidden_bias(j, HALF)
         gelu_store(j, HALF, N_TILE)

@@ -92,9 +92,9 @@ def tile_swablock_pb_kernel(tc, x, o_heads, Wo, bo, gamma, beta, W1, b1, out_0, 
                             in_=Wo[k0 : k0 + 2 * P, cols].rearrange("(q e) c -> q e c", e=2),
                         )
 
-        def load_w1(first):
+        def load_w1(first, passes):
             cols = slice(first, first + HALF)
-            for g in range(PASSES):
+            for g in passes:
                 nc.sync.dma_start(
                     out=w1_raw[first // HALF][:, g, :, :],
                     in_=W1[g * K_PASS : (g + 1) * K_PASS, cols].rearrange("(t p) n -> p t n", p=P),
@@ -102,11 +102,14 @@ def tile_swablock_pb_kernel(tc, x, o_heads, Wo, bo, gamma, beta, W1, b1, out_0, 
 
         load_wo()
         nc.sync.dma_start(out=x_all[:, 0, :], in_=x_tiles[0])
-        load_tokens(1)
+        load_w1(0, [0])
+        nc.sync.dma_start(out=o_all[:, 1, :], in_=o_tiles[1])
+        load_w1(0, [1])
+        nc.sync.dma_start(out=x_all[:, 1, :], in_=x_tiles[1])
         load_tokens(2)
-        load_w1(0)
+        load_w1(HALF, [0])
         load_tokens(3)
-        load_w1(HALF)
+        load_w1(HALF, [1])
         for j in range(4, TOKEN_TILES):
             load_tokens(j)
             if j == 6:
@@ -325,21 +328,37 @@ def tile_swablock_pb_kernel(tc, x, o_heads, Wo, bo, gamma, beta, W1, b1, out_0, 
         quantise(wo10, wo_codes, wo_scales)
         bias_residual(0)
         copy_biased(0)
+        project(0)
+
+        pieces = {}
+        pieces[0, 0] = regroup(w1_raw, 0, 0, nc.vector.tensor_copy)
+        pieces[0, 1] = regroup(w1_raw, 0, 1, nc.scalar.copy)
+        add_residual(0)
+        mean(0)
+        sum_squares(0)
+        inverse_std(0)
+        pieces[1, 0] = regroup(w1_raw, 1, 0, nc.vector.tensor_copy)
+        centre(0)
         flip_heads(1)
         copy_heads(1)
-        project(0)
         bias_residual(1)
         copy_biased(1)
+        quantise(pieces.pop((0, 0)), w1_codes, w1_scales)
+        quantise_heads(1)
+        project(1)
+        pieces[1, 1] = regroup(w1_raw, 1, 1, nc.scalar.copy)
         flip_heads(2)
+        copy_heads(2)
         bias_residual(2)
+        quantise(pieces.pop((0, 1)), w1_codes, w1_scales)
+        quantise(pieces.pop((1, 0)), w1_codes, w1_scales)
 
-        PLAN_V = {0: [(0,0),(1,0)], 1: [(0,2),(1,2)]}
-        PLAN_S = {0: [(0,1),(1,1)], 1: [(0,3),(1,3)]}
-        PLAN_QA = {1: [(0,1),(1,1),(0,2),(1,2)]}
-        PLAN_Q = {0: [(0,0),(1,0)], 1: [(0,3)]}
+        PLAN_V = {1: [(0,2),(1,2)]}
+        PLAN_S = {1: [(0,3),(1,3)]}
+        PLAN_QA = {1: [(1,1),(0,2),(1,2)]}
+        PLAN_Q = {1: [(0,3)]}
         PLAN_Q0 = {2: [(1,3)]}
-        pieces = {}
-        for i in range(TOKEN_TILES - 1):
+        for i in range(1, TOKEN_TILES - 1):
             in_range(add_residual, i)
             for name in PLAN_Q0.get(i, []):
                 quantise(pieces.pop(name), w1_codes, w1_scales)
@@ -347,19 +366,17 @@ def tile_swablock_pb_kernel(tc, x, o_heads, Wo, bo, gamma, beta, W1, b1, out_0, 
             in_range(quantise_heads, i + 1)
             in_range(mean, i)
             in_range(sum_squares, i)
-            if i == 0:
-                copy_heads(2)
             in_range(inverse_std, i)
             in_range(normalise, i - 1)
-            in_range(copy_biased, i + 2)
+            in_range(copy_biased, i + 1)
             in_range(flip_normed, i - 1)
             in_range(copy_normed, i - 1)
-            if i > 0:
-                in_range(flip_heads, i + 3)
+            in_range(flip_heads, i + 2)
+            in_range(copy_heads, i + 2)
             in_range(add_hidden_bias, i - LAG, 0)
             in_range(gelu_store, i - LAG, 0)
             in_range(project, i + 1)
-            in_range(bias_residual, i + 3)
+            in_range(bias_residual, i + 2)
             in_range(add_hidden_bias, i - LAG, HALF)
             in_range(centre, i)
             for g, n in PLAN_V.get(i, []):
@@ -367,9 +384,6 @@ def tile_swablock_pb_kernel(tc, x, o_heads, Wo, bo, gamma, beta, W1, b1, out_0, 
             in_range(gelu_store, i - LAG, HALF)
             for g, n in PLAN_S.get(i, []):
                 pieces[g, n] = regroup(w1_raw, g, n, nc.scalar.copy)
-            if i == 0:
-                flip_heads(3)
-            in_range(copy_heads, i + 3)
             for name in PLAN_QA.get(i, []):
                 quantise(pieces.pop(name), w1_codes, w1_scales)
             in_range(quantise_normed, i - 1)

@@ -292,15 +292,18 @@ def tile_swablock_pb_kernel(tc, x, o_heads, Wo, bo, gamma, beta, W1, b1, out_0, 
                 sums.append(acc)
             live["hidden_sums", j, first] = sums
 
-        def add_hidden_bias(j, first):
-            hidden = work.tile([P, HALF], F32, tag="hidden", bufs=6)
-            for n, acc in enumerate(live.pop(("hidden_sums", j, first))):
+        def add_hidden_bias(j, first, banks=range(HALF // N_TILE)):
+            if ("hidden", j, first) not in live:
+                hidden = work.tile([P, HALF], F32, tag="hidden", bufs=6)
+                live["hidden", j, first] = hidden
+            hidden = live["hidden", j, first]
+            for n in banks:
+                acc = live["hidden_sums", j, first][n]
                 start = first + n * N_TILE
                 nc.vector.tensor_tensor(
                     out=hidden[:, n * N_TILE : (n + 1) * N_TILE], in0=acc[:],
                     in1=b1_all[:, start : start + N_TILE], op=ALU.add,
                 )
-            live["hidden", j, first] = hidden
 
         def gelu_store(j, first, width=HALF):
             hidden = live.pop(("hidden", j, first))
@@ -322,8 +325,8 @@ def tile_swablock_pb_kernel(tc, x, o_heads, Wo, bo, gamma, beta, W1, b1, out_0, 
         quantise(wo00, wo_codes, wo_scales)
         quantise(wo01, wo_codes, wo_scales)
         wo10 = regroup(wo_raw, 1, 0, nc.scalar.copy)
-        wo11 = regroup(wo_raw, 1, 1, nc.vector.tensor_copy)
         quantise_heads(0)
+        wo11 = regroup(wo_raw, 1, 1, nc.vector.tensor_copy)
         quantise(wo11, wo_codes, wo_scales)
         quantise(wo10, wo_codes, wo_scales)
         bias_residual(0)
@@ -401,9 +404,10 @@ def tile_swablock_pb_kernel(tc, x, o_heads, Wo, bo, gamma, beta, W1, b1, out_0, 
         flip_normed(j - 1)
         copy_normed(j - 1)
         centre(j)
+        add_hidden_bias(j - 2, 0, [0])
         normalise(j)
         flip_normed(j)
-        add_hidden_bias(j - 2, 0)
+        add_hidden_bias(j - 2, 0, [1])
         quantise_normed(j - 1)
         hidden_matmuls(j - 1, 0)
         copy_normed(j, (nc.scalar.copy, nc.vector.tensor_copy))

@@ -52,7 +52,6 @@ def tile_swablock_pb_kernel(tc, x, o_heads, Wo, bo, gamma, beta, W1, b1, out_0, 
         nc.scalar.dma_start(out=vector_rows[0:1, :], in_=bo.unsqueeze(0))
         nc.scalar.dma_start(out=vector_rows[1:2, :], in_=gamma.unsqueeze(0))
         nc.scalar.dma_start(out=vector_rows[2:3, :], in_=beta.unsqueeze(0))
-        nc.scalar.dma_start(out=vector_rows[3:5, :], in_=b1.rearrange("(a c) -> a c", a=2))
         warm = keep.tile([P, 1], F32)
         nc.scalar.activation(out=warm[:], in_=neg_half[:], func=ACT.Gelu)
 
@@ -64,11 +63,13 @@ def tile_swablock_pb_kernel(tc, x, o_heads, Wo, bo, gamma, beta, W1, b1, out_0, 
         b1_all = keep.tile([P, F], BF16)
 
         def spread_row(j, copy, dst):
+            bank = psum.tile([P, D], BF16, tag="acc")
             for n in range(D // N_TILE):
                 cols = slice(n * N_TILE, (n + 1) * N_TILE)
-                acc = psum.tile([P, N_TILE], F32, tag="acc")
-                nc.tensor.matmul(out=acc[:], lhsT=row_selector(j), rhs=vector_rows[:, cols], start=True, stop=True)
-                copy(out=dst[:, cols], in_=acc[:])
+                nc.tensor.matmul(
+                    out=bank[:, cols], lhsT=row_selector(j), rhs=vector_rows[:, cols], start=True, stop=True
+                )
+            copy(out=dst[:], in_=bank[:])
 
         o_all = keep.tile([P, TOKEN_TILES, D], BF16)
         x_all = keep.tile([P, TOKEN_TILES, D], BF16)
@@ -318,13 +319,13 @@ def tile_swablock_pb_kernel(tc, x, o_heads, Wo, bo, gamma, beta, W1, b1, out_0, 
 
         flip_heads(0)
         copy_heads(0)
-        spread_row(1, nc.scalar.copy, gamma_all)
-        spread_row(2, nc.scalar.copy, beta_all)
         wo00 = regroup(wo_raw, 0, 0, nc.vector.tensor_copy)
         wo01 = regroup(wo_raw, 0, 1, nc.vector.tensor_copy)
         quantise(wo00, wo_codes, wo_scales)
         quantise(wo01, wo_codes, wo_scales)
         wo10 = regroup(wo_raw, 1, 0, nc.scalar.copy)
+        spread_row(1, nc.scalar.copy, gamma_all)
+        spread_row(2, nc.scalar.copy, beta_all)
         quantise_heads(0)
         wo11 = regroup(wo_raw, 1, 1, nc.vector.tensor_copy)
         quantise(wo11, wo_codes, wo_scales)

@@ -105,8 +105,8 @@ def tile_swablock_pb_kernel(tc, x, o_heads, Wo, bo, gamma, beta, W1, b1, out_0, 
         nc.sync.dma_start(out=x_all[:, 0, :], in_=x_tiles[0])
         load_w1(0, [0])
         nc.sync.dma_start(out=o_all[:, 1, :], in_=o_tiles[1])
-        load_w1(0, [1])
         nc.sync.dma_start(out=x_all[:, 1, :], in_=x_tiles[1])
+        load_w1(0, [1])
         load_tokens(2)
         load_w1(HALF, [0])
         load_tokens(3)
@@ -337,41 +337,41 @@ def tile_swablock_pb_kernel(tc, x, o_heads, Wo, bo, gamma, beta, W1, b1, out_0, 
         pieces = {}
         pieces[0, 0] = regroup(w1_raw, 0, 0, nc.vector.tensor_copy)
         pieces[0, 1] = regroup(w1_raw, 0, 1, nc.scalar.copy)
+        flip_heads(1)
         add_residual(0)
         mean(0)
         sum_squares(0)
         inverse_std(0)
-        pieces[1, 0] = regroup(w1_raw, 1, 0, nc.vector.tensor_copy)
-        centre(0)
-        flip_heads(1)
         copy_heads(1)
+        quantise(pieces.pop((0, 0)), w1_codes, w1_scales)
+        centre(0)
+        quantise_heads(1)
+        pieces[1, 0] = regroup(w1_raw, 1, 0, nc.vector.tensor_copy)
+        pieces[1, 1] = regroup(w1_raw, 1, 1, nc.scalar.copy)
         bias_residual(1)
         copy_biased(1)
-        quantise(pieces.pop((0, 0)), w1_codes, w1_scales)
-        quantise_heads(1)
         project(1)
-        pieces[1, 1] = regroup(w1_raw, 1, 1, nc.scalar.copy)
+        quantise(pieces.pop((0, 1)), w1_codes, w1_scales)
+        quantise(pieces.pop((1, 0)), w1_codes, w1_scales)
         flip_heads(2)
         copy_heads(2)
         bias_residual(2)
-        quantise(pieces.pop((0, 1)), w1_codes, w1_scales)
-        quantise(pieces.pop((1, 0)), w1_codes, w1_scales)
 
         PLAN_V = {1: [(0,2),(1,2)]}
         PLAN_S = {1: [(0,3),(1,3)]}
         PLAN_QA = {1: [(1,1),(0,2),(1,2)]}
-        PLAN_Q = {1: [(0,3)]}
-        PLAN_Q0 = {2: [(1,3)]}
+        PLAN_Q = {}
+        PLAN_Q0 = {2: [(0,3),(1,3)]}
         for i in range(1, TOKEN_TILES - 1):
             in_range(add_residual, i)
-            for name in PLAN_Q0.get(i, []):
-                quantise(pieces.pop(name), w1_codes, w1_scales)
-            in_range(hidden_matmuls, i - LAG, HALF)
             in_range(quantise_heads, i + 1)
             in_range(mean, i)
             in_range(sum_squares, i)
             in_range(inverse_std, i)
             in_range(normalise, i - 1)
+            for name in PLAN_Q0.get(i, []):
+                quantise(pieces.pop(name), w1_codes, w1_scales)
+            in_range(hidden_matmuls, i - LAG, HALF)
             in_range(copy_biased, i + 1)
             in_range(flip_normed, i - 1)
             in_range(copy_normed, i - 1)
@@ -397,28 +397,28 @@ def tile_swablock_pb_kernel(tc, x, o_heads, Wo, bo, gamma, beta, W1, b1, out_0, 
 
         j = TOKEN_TILES - 1
         add_residual(j)
-        hidden_matmuls(j - 2, HALF)
         mean(j)
         sum_squares(j)
         inverse_std(j)
         normalise(j - 1)
         flip_normed(j - 1)
         copy_normed(j - 1)
+        hidden_matmuls(j - 2, HALF)
         centre(j)
-        add_hidden_bias(j - 2, 0, [0])
-        normalise(j)
-        flip_normed(j)
-        add_hidden_bias(j - 2, 0, [1])
+        add_hidden_bias(j - 2, 0)
+        gelu_store(j - 2, 0)
         quantise_normed(j - 1)
         hidden_matmuls(j - 1, 0)
-        copy_normed(j, (nc.scalar.copy, nc.vector.tensor_copy))
-        gelu_store(j - 2, 0)
+        normalise(j)
+        flip_normed(j)
         add_hidden_bias(j - 2, HALF)
-        gelu_store(j - 2, HALF)
         hidden_matmuls(j - 1, HALF)
-        add_hidden_bias(j - 1, 0)
-        gelu_store(j - 1, 0)
+        add_hidden_bias(j - 1, 0, [0])
+        copy_normed(j, (nc.scalar.copy, nc.vector.tensor_copy))
+        gelu_store(j - 2, HALF)
+        add_hidden_bias(j - 1, 0, [1])
         quantise_normed(j)
+        gelu_store(j - 1, 0)
         hidden_matmuls(j, 0)
         add_hidden_bias(j - 1, HALF)
         gelu_store(j - 1, HALF, N_TILE)

@@ -185,11 +185,12 @@ def tile_swablock_pb_kernel(tc, x, o_heads, Wo, bo, gamma, beta, W1, b1, out_0, 
                 sums.append(xb_sum)
             live["xb_sums", j] = sums
 
-        def copy_biased(j):
-            xb = work.tile([P, D], F32, tag="xb")
-            for n, xb_sum in enumerate(live.pop(("xb_sums", j))):
-                nc.scalar.copy(out=xb[:, n * N_TILE : (n + 1) * N_TILE], in_=xb_sum[:])
-            live["xb", j] = xb
+        def copy_biased(j, banks=range(D // N_TILE)):
+            if ("xb", j) not in live:
+                xb = work.tile([P, D], F32, tag="xb")
+                live["xb", j] = xb
+            for n in banks:
+                nc.scalar.copy(out=live["xb", j][:, n * N_TILE : (n + 1) * N_TILE], in_=live["xb_sums", j][n][:])
 
         def project(j):
             codes, scales = live.pop(("o_mx", j))
@@ -294,24 +295,25 @@ def tile_swablock_pb_kernel(tc, x, o_heads, Wo, bo, gamma, beta, W1, b1, out_0, 
             live["hidden_sums", j, first] = sums
 
         def add_hidden_bias(j, first, banks=range(HALF // N_TILE)):
-            if ("hidden", j, first) not in live:
-                hidden = work.tile([P, HALF], F32, tag="hidden", bufs=6)
-                live["hidden", j, first] = hidden
-            hidden = live["hidden", j, first]
+            if ("hidden", j) not in live:
+                hidden = work.tile([P, F], F32, tag="hidden", bufs=3)
+                live["hidden", j] = hidden
+            hidden = live["hidden", j]
             for n in banks:
                 acc = live["hidden_sums", j, first][n]
                 start = first + n * N_TILE
                 nc.vector.tensor_tensor(
-                    out=hidden[:, n * N_TILE : (n + 1) * N_TILE], in0=acc[:],
+                    out=hidden[:, start : start + N_TILE], in0=acc[:],
                     in1=b1_all[:, start : start + N_TILE], op=ALU.add,
                 )
 
-        def gelu_store(j, first, width=HALF):
-            hidden = live.pop(("hidden", j, first))
-            for c in range(0, HALF, width):
+        def gelu_store(j, first, width=HALF, last=None):
+            last = first + HALF if last is None else last
+            hidden = live["hidden", j]
+            for c in range(first, last, width):
                 piece = hidden[:, c : c + width]
                 nc.scalar.activation(out=piece, in_=piece, func=ACT.Gelu)
-                nc.sync.dma_start(out=h_tiles[j][:, first + c : first + c + width], in_=piece)
+                nc.sync.dma_start(out=h_tiles[j][:, c : c + width], in_=piece)
 
         def in_range(stage, j, *args):
             if 0 <= j < TOKEN_TILES:
@@ -328,8 +330,8 @@ def tile_swablock_pb_kernel(tc, x, o_heads, Wo, bo, gamma, beta, W1, b1, out_0, 
         spread_row(2, nc.scalar.copy, beta_all)
         quantise_heads(0)
         wo11 = regroup(wo_raw, 1, 1, nc.vector.tensor_copy)
-        quantise(wo11, wo_codes, wo_scales)
         quantise(wo10, wo_codes, wo_scales)
+        quantise(wo11, wo_codes, wo_scales)
         bias_residual(0)
         copy_biased(0)
         project(0)
@@ -340,19 +342,19 @@ def tile_swablock_pb_kernel(tc, x, o_heads, Wo, bo, gamma, beta, W1, b1, out_0, 
         flip_heads(1)
         add_residual(0)
         mean(0)
+        copy_heads(1)
         sum_squares(0)
         inverse_std(0)
-        copy_heads(1)
         quantise(pieces.pop((0, 0)), w1_codes, w1_scales)
         centre(0)
         quantise_heads(1)
         pieces[1, 0] = regroup(w1_raw, 1, 0, nc.vector.tensor_copy)
-        pieces[1, 1] = regroup(w1_raw, 1, 1, nc.scalar.copy)
         bias_residual(1)
         copy_biased(1)
         project(1)
         quantise(pieces.pop((0, 1)), w1_codes, w1_scales)
         quantise(pieces.pop((1, 0)), w1_codes, w1_scales)
+        pieces[1, 1] = regroup(w1_raw, 1, 1, nc.scalar.copy)
         flip_heads(2)
         copy_heads(2)
         bias_residual(2)
@@ -366,26 +368,26 @@ def tile_swablock_pb_kernel(tc, x, o_heads, Wo, bo, gamma, beta, W1, b1, out_0, 
             in_range(add_residual, i)
             in_range(quantise_heads, i + 1)
             in_range(mean, i)
+            in_range(copy_biased, i + 1, [0])
             in_range(sum_squares, i)
             in_range(inverse_std, i)
+            in_range(copy_biased, i + 1, [1])
             in_range(normalise, i - 1)
             for name in PLAN_Q0.get(i, []):
                 quantise(pieces.pop(name), w1_codes, w1_scales)
             in_range(hidden_matmuls, i - LAG, HALF)
-            in_range(copy_biased, i + 1)
             in_range(flip_normed, i - 1)
             in_range(copy_normed, i - 1)
             in_range(flip_heads, i + 2)
             in_range(copy_heads, i + 2)
             in_range(add_hidden_bias, i - LAG, 0)
-            in_range(gelu_store, i - LAG, 0)
             in_range(project, i + 1)
             in_range(bias_residual, i + 2)
             in_range(add_hidden_bias, i - LAG, HALF)
             in_range(centre, i)
             for g, n in PLAN_V.get(i, []):
                 pieces[g, n] = regroup(w1_raw, g, n, nc.vector.tensor_copy)
-            in_range(gelu_store, i - LAG, HALF)
+            in_range(gelu_store, i - LAG, 0, F, F)
             for g, n in PLAN_S.get(i, []):
                 pieces[g, n] = regroup(w1_raw, g, n, nc.scalar.copy)
             for name in PLAN_QA.get(i, []):
@@ -404,21 +406,22 @@ def tile_swablock_pb_kernel(tc, x, o_heads, Wo, bo, gamma, beta, W1, b1, out_0, 
         flip_normed(j - 1)
         copy_normed(j - 1)
         hidden_matmuls(j - 2, HALF)
-        centre(j)
         add_hidden_bias(j - 2, 0)
+        centre(j)
         gelu_store(j - 2, 0)
         quantise_normed(j - 1)
         hidden_matmuls(j - 1, 0)
+        add_hidden_bias(j - 2, HALF, [0])
+        gelu_store(j - 2, HALF, N_TILE, HALF + N_TILE)
         normalise(j)
         flip_normed(j)
-        add_hidden_bias(j - 2, HALF)
+        add_hidden_bias(j - 2, HALF, [1])
         hidden_matmuls(j - 1, HALF)
-        add_hidden_bias(j - 1, 0, [0])
+        gelu_store(j - 2, HALF + N_TILE, N_TILE, F)
+        add_hidden_bias(j - 1, 0)
         copy_normed(j, (nc.scalar.copy, nc.vector.tensor_copy))
-        gelu_store(j - 2, HALF)
-        add_hidden_bias(j - 1, 0, [1])
-        quantise_normed(j)
         gelu_store(j - 1, 0)
+        quantise_normed(j)
         hidden_matmuls(j, 0)
         add_hidden_bias(j - 1, HALF)
         gelu_store(j - 1, HALF, N_TILE)

@@ -73,7 +73,7 @@ def tile_swablock_pb_kernel(tc, x, o_heads, Wo, bo, gamma, beta, W1, b1, out_0, 
 
         o_all = keep.tile([P, TOKEN_TILES, D], BF16)
         x_all = keep.tile([P, TOKEN_TILES, D], BF16)
-        wo_raw = [keep.tile([P, PASSES, PACK, N_TILE], BF16, name="wo_raw%d" % n) for n in range(D // N_TILE)]
+        wo_raw = keep.tile([P, PASSES, 2, 2 * D], BF16)
         w1_raw = [keep.tile([P, PASSES, PACK, HALF], BF16, name="w1_raw%d" % n) for n in range(F // HALF)]
 
         def load_tokens(j):
@@ -82,16 +82,13 @@ def tile_swablock_pb_kernel(tc, x, o_heads, Wo, bo, gamma, beta, W1, b1, out_0, 
 
         def load_wo():
             for g in range(PASSES):
-                for n in range(D // N_TILE):
-                    if (g, n) == (0, 1):
-                        nc.sync.dma_start(out=o_all[:, 0, :], in_=o_tiles[0])
-                    cols = slice(n * N_TILE, (n + 1) * N_TILE)
-                    for u in range(2):
-                        k0 = g * K_PASS + u * 2 * P
-                        nc.sync.dma_start(
-                            out=wo_raw[n][:, g, 2 * u : 2 * u + 2, :],
-                            in_=Wo[k0 : k0 + 2 * P, cols].rearrange("(q e) c -> q e c", e=2),
-                        )
+                for u in range(2):
+                    k0 = g * K_PASS + u * 2 * P
+                    nc.sync.dma_start(
+                        out=wo_raw[:, g, u, :], in_=Wo[k0 : k0 + 2 * P, :].rearrange("(q e) c -> q (e c)", e=2)
+                    )
+                if g == 0:
+                    nc.sync.dma_start(out=o_all[:, 0, :], in_=o_tiles[0])
 
         def load_w1(first, passes):
             cols = slice(first, first + HALF)
@@ -121,16 +118,24 @@ def tile_swablock_pb_kernel(tc, x, o_heads, Wo, bo, gamma, beta, W1, b1, out_0, 
         w1_codes = keep.tile([P, PASSES, F], U32, align_bytes=64)
         w1_scales = keep.tile([P, PASSES, F], U8, align_bytes=64)
 
-        def regroup(raw_tiles, g, n, copy):
+        def wo_rows(g, n):
+            return wo_raw[:, g, :, :].rearrange("p u (e c) -> p (u e) c", e=2)[:, :, n * N_TILE : (n + 1) * N_TILE]
+
+        def w1_rows(g, n):
+            first = n * N_TILE % HALF
+            return w1_raw[n * N_TILE // HALF][:, g, :, first : first + N_TILE]
+
+        def regroup(rows, g, n, copy):
             cols = slice(n * N_TILE, (n + 1) * N_TILE)
-            tile_cols = raw_tiles[0].shape[3]
-            raw = raw_tiles[n * N_TILE // tile_cols]
-            first = n * N_TILE % tile_cols
             grouped = work.tile([P, N_TILE * PACK], BF16, align_bytes=64, tag="w_grouped", bufs=5)
-            copy(
-                out=grouped[:].rearrange("p (c i t) -> p c t i", i=4, t=PACK),
-                in_=raw[:, g, :, first : first + N_TILE].rearrange("p t (c i) -> p c t i", i=4),
-            )
+            copies = copy if isinstance(copy, tuple) else (copy,)
+            width = N_TILE // len(copies)
+            for h, part in enumerate(copies):
+                c0 = h * width
+                part(
+                    out=grouped[:, c0 * PACK : (c0 + width) * PACK].rearrange("p (c i t) -> p c t i", i=4, t=PACK),
+                    in_=rows(g, n)[:, :, c0 : c0 + width].rearrange("p t (c i) -> p c t i", i=4),
+                )
             return grouped, g, cols
 
         def quantise(piece, codes, scales):
@@ -321,15 +326,15 @@ def tile_swablock_pb_kernel(tc, x, o_heads, Wo, bo, gamma, beta, W1, b1, out_0, 
 
         flip_heads(0)
         copy_heads(0)
-        wo00 = regroup(wo_raw, 0, 0, nc.vector.tensor_copy)
-        wo01 = regroup(wo_raw, 0, 1, nc.vector.tensor_copy)
+        wo00 = regroup(wo_rows, 0, 0, nc.vector.tensor_copy)
+        wo01 = regroup(wo_rows, 0, 1, nc.vector.tensor_copy)
         quantise(wo00, wo_codes, wo_scales)
         quantise(wo01, wo_codes, wo_scales)
-        wo10 = regroup(wo_raw, 1, 0, nc.scalar.copy)
+        wo10 = regroup(wo_rows, 1, 0, (nc.vector.tensor_copy, nc.scalar.copy))
         spread_row(1, nc.scalar.copy, gamma_all)
         spread_row(2, nc.scalar.copy, beta_all)
         quantise_heads(0)
-        wo11 = regroup(wo_raw, 1, 1, nc.vector.tensor_copy)
+        wo11 = regroup(wo_rows, 1, 1, nc.vector.tensor_copy)
         quantise(wo10, wo_codes, wo_scales)
         quantise(wo11, wo_codes, wo_scales)
         bias_residual(0)
@@ -337,8 +342,8 @@ def tile_swablock_pb_kernel(tc, x, o_heads, Wo, bo, gamma, beta, W1, b1, out_0, 
         project(0)
 
         pieces = {}
-        pieces[0, 0] = regroup(w1_raw, 0, 0, nc.vector.tensor_copy)
-        pieces[0, 1] = regroup(w1_raw, 0, 1, nc.scalar.copy)
+        pieces[0, 0] = regroup(w1_rows, 0, 0, nc.vector.tensor_copy)
+        pieces[0, 1] = regroup(w1_rows, 0, 1, nc.scalar.copy)
         flip_heads(1)
         add_residual(0)
         mean(0)
@@ -348,13 +353,13 @@ def tile_swablock_pb_kernel(tc, x, o_heads, Wo, bo, gamma, beta, W1, b1, out_0, 
         quantise(pieces.pop((0, 0)), w1_codes, w1_scales)
         centre(0)
         quantise_heads(1)
-        pieces[1, 0] = regroup(w1_raw, 1, 0, nc.vector.tensor_copy)
+        pieces[1, 0] = regroup(w1_rows, 1, 0, nc.vector.tensor_copy)
         bias_residual(1)
         copy_biased(1)
         project(1)
         quantise(pieces.pop((0, 1)), w1_codes, w1_scales)
         quantise(pieces.pop((1, 0)), w1_codes, w1_scales)
-        pieces[1, 1] = regroup(w1_raw, 1, 1, nc.scalar.copy)
+        pieces[1, 1] = regroup(w1_rows, 1, 1, nc.scalar.copy)
         flip_heads(2)
         copy_heads(2)
         bias_residual(2)
@@ -386,10 +391,10 @@ def tile_swablock_pb_kernel(tc, x, o_heads, Wo, bo, gamma, beta, W1, b1, out_0, 
             in_range(add_hidden_bias, i - LAG, HALF)
             in_range(centre, i)
             for g, n in PLAN_V.get(i, []):
-                pieces[g, n] = regroup(w1_raw, g, n, nc.vector.tensor_copy)
+                pieces[g, n] = regroup(w1_rows, g, n, nc.vector.tensor_copy)
             in_range(gelu_store, i - LAG, 0, F, F)
             for g, n in PLAN_S.get(i, []):
-                pieces[g, n] = regroup(w1_raw, g, n, nc.scalar.copy)
+                pieces[g, n] = regroup(w1_rows, g, n, nc.scalar.copy)
             for name in PLAN_QA.get(i, []):
                 quantise(pieces.pop(name), w1_codes, w1_scales)
             in_range(quantise_normed, i - 1)

from contextlib import ExitStack

import concourse.mybir as mybir
from concourse.masks import make_identity

F32 = mybir.dt.float32
BF16 = mybir.dt.bfloat16
U32 = mybir.dt.uint32
U8 = mybir.dt.uint8
FP8X4 = mybir.dt.float8_e4m3fn_x4
ALU = mybir.AluOpType
ACT = mybir.ActivationFunctionType

S, D, F = 1536, 1024, 2048
EPS = 1e-5
P = 128
PACK = 4
K_PASS = P * PACK
PASSES = D // K_PASS
N_TILE = 512
HALF = 2 * N_TILE
TOKEN_TILES = S // P
LAG = 2

assert LAG * HALF == F

FLOPS = 2 * S * D * D + 2 * S * D * F


def tile_swablock_pb_kernel(tc, x, o_heads, Wo, bo, gamma, beta, W1, b1, out_0, out_1):
    nc = tc.nc
    x_tiles = x.flatten_outer_dims().rearrange("(n p) d -> n p d", p=P)
    o_tiles = o_heads.flatten_outer_dims().rearrange("(n p) d -> n p d", p=P)
    xn_tiles = out_0.flatten_outer_dims().rearrange("(n p) d -> n p d", p=P)
    h_tiles = out_1.flatten_outer_dims().rearrange("(n p) f -> n p f", p=P)

    with ExitStack() as ctx:
        ctx.enter_context(tc.manual_schedule())
        keep = ctx.enter_context(tc.tile_pool(name="keep", bufs=1))
        work = ctx.enter_context(tc.tile_pool(name="work", bufs=2))
        psum = ctx.enter_context(tc.psum_pool(name="psum", bufs=4))

        ident_f32 = keep.tile([P, P], F32)
        make_identity(nc, ident_f32[:])
        ident_bf16 = keep.tile([P, P], BF16)
        make_identity(nc, ident_bf16[:])
        neg_half = keep.tile([P, 1], F32)
        nc.vector.memset(neg_half[:], -0.5)

        vector_rows = keep.tile([P, D], BF16)
        nc.vector.memset(vector_rows[:].bitcast(U32), 0)
        nc.scalar.dma_start(out=vector_rows[0:1, :], in_=bo.unsqueeze(0))
        nc.scalar.dma_start(out=vector_rows[1:2, :], in_=gamma.unsqueeze(0))
        nc.scalar.dma_start(out=vector_rows[2:3, :], in_=beta.unsqueeze(0))
        warm = keep.tile([P, 1], F32)
        nc.scalar.activation(out=warm[:], in_=neg_half[:], func=ACT.Gelu)

        def row_selector(j):
            return ident_bf16[:, j : j + 1].to_broadcast([P, P])

        gamma_all = keep.tile([P, D], BF16)
        beta_all = keep.tile([P, D], BF16)
        b1_all = keep.tile([P, F], BF16)

        def spread_row(j, copy, dst):
            bank = psum.tile([P, D], BF16, tag="acc")
            for n in range(D // N_TILE):
                cols = slice(n * N_TILE, (n + 1) * N_TILE)
                nc.tensor.matmul(
                    out=bank[:, cols], lhsT=row_selector(j), rhs=vector_rows[:, cols], start=True, stop=True
                )
            copy(out=dst[:], in_=bank[:])

        o_all = keep.tile([P, TOKEN_TILES, D], BF16)
        x_all = keep.tile([P, TOKEN_TILES, D], BF16)
        wo_raw = keep.tile([P, PASSES, 2, 2 * D], BF16)
        w1_raw = [keep.tile([P, PASSES, PACK, HALF], BF16, name="w1_raw%d" % n) for n in range(F // HALF)]

        def load_tokens(j):
            nc.sync.dma_start(out=o_all[:, j, :], in_=o_tiles[j])
            nc.sync.dma_start(out=x_all[:, j, :], in_=x_tiles[j])

        def load_wo():
            for g in range(PASSES):
                for u in range(2):
                    k0 = g * K_PASS + u * 2 * P
                    nc.sync.dma_start(
                        out=wo_raw[:, g, u, :], in_=Wo[k0 : k0 + 2 * P, :].rearrange("(q e) c -> q (e c)", e=2)
                    )
                if g == 0:
                    nc.sync.dma_start(out=o_all[:, 0, :], in_=o_tiles[0])

        def load_w1(first, passes):
            cols = slice(first, first + HALF)
            for g in passes:
                nc.sync.dma_start(
                    out=w1_raw[first // HALF][:, g, :, :],
                    in_=W1[g * K_PASS : (g + 1) * K_PASS, cols].rearrange("(t p) n -> p t n", p=P),
                )

        load_wo()
        nc.sync.dma_start(out=x_all[:, 0, :], in_=x_tiles[0])
        load_w1(0, [0])
        nc.sync.dma_start(out=o_all[:, 1, :], in_=o_tiles[1])
        nc.sync.dma_start(out=x_all[:, 1, :], in_=x_tiles[1])
        load_w1(0, [1])
        load_tokens(2)
        load_w1(HALF, [0])
        load_tokens(3)
        load_w1(HALF, [1])
        for j in range(4, TOKEN_TILES):
            load_tokens(j)
            if j == 6:
                nc.sync.dma_start(out=b1_all[:], in_=b1.partition_broadcast(P))

        wo_codes = keep.tile([P, PASSES, D], U32, align_bytes=64)
        wo_scales = keep.tile([P, PASSES, D], U8, align_bytes=64)
        w1_codes = keep.tile([P, PASSES, F], U32, align_bytes=64)
        w1_scales = keep.tile([P, PASSES, F], U8, align_bytes=64)

        def wo_rows(g, n):
            return wo_raw[:, g, :, :].rearrange("p u (e c) -> p (u e) c", e=2)[:, :, n * N_TILE : (n + 1) * N_TILE]

        def w1_rows(g, n):
            first = n * N_TILE % HALF
            return w1_raw[n * N_TILE // HALF][:, g, :, first : first + N_TILE]

        def regroup(rows, g, n, copy):
            cols = slice(n * N_TILE, (n + 1) * N_TILE)
            grouped = work.tile([P, N_TILE * PACK], BF16, align_bytes=64, tag="w_grouped", bufs=5)
            copies = copy if isinstance(copy, tuple) else (copy,)
            width = N_TILE // len(copies)
            for h, part in enumerate(copies):
                c0 = h * width
                part(
                    out=grouped[:, c0 * PACK : (c0 + width) * PACK].rearrange("p (c i t) -> p c t i", i=4, t=PACK),
                    in_=rows(g, n)[:, :, c0 : c0 + width].rearrange("p t (c i) -> p c t i", i=4),
                )
            return grouped, g, cols

        def quantise(piece, codes, scales):
            grouped, g, cols = piece
            nc.vector.quantize_mx(out=codes[:, g, cols].bitcast(FP8X4), scales=scales[:, g, cols], in_=grouped[:])

        def mx_group(acc, codes, scales, w_codes, w_scales, cols):
            for g in range(PASSES):
                toks = slice(g * P, (g + 1) * P)
                nc.tensor.matmul_mx(
                    out=acc[:],
                    lhsT=codes[:, toks].bitcast(FP8X4),
                    lhsT_scale=scales[:, toks],
                    rhs=w_codes[:, g, cols].bitcast(FP8X4),
                    rhs_scale=w_scales[:, g, cols],
                    start=(g == 0),
                    stop=(g == PASSES - 1),
                )

        live = {}

        def flip_heads(j):
            words = o_all[:, j, :].bitcast(F32)
            flipped = psum.tile([P, PASSES * 2, P], F32, tag="flipped")
            for a in range(PASSES * 2):
                nc.tensor.transpose(flipped[:, a, :], words[:, a * P : (a + 1) * P], ident_f32[:])
            live["o_flipped", j] = flipped

        def copy_heads(j):
            flipped = live.pop(("o_flipped", j))
            grouped = work.tile([P, D], BF16, align_bytes=64, tag="o_grouped")
            nc.scalar.copy(
                out=grouped[:].bitcast(F32).rearrange("p (g r u) -> p g r u", g=PASSES, u=2),
                in_=flipped[:].rearrange("p (g u) r -> p g r u", u=2),
            )
            live["o_grouped", j] = grouped

        def quantise_heads(j):
            grouped = live.pop(("o_grouped", j))
            codes = work.tile([P, PASSES * P], U32, align_bytes=64, tag="o_codes")
            scales = work.tile([P, PASSES * P], U8, align_bytes=64, tag="o_scales")
            nc.vector.quantize_mx(out=codes[:].bitcast(FP8X4), scales=scales[:], in_=grouped[:])
            live["o_mx", j] = (codes, scales)

        def bias_residual(j):
            sums = []
            for n in range(D // N_TILE):
                cols = slice(n * N_TILE, (n + 1) * N_TILE)
                xb_sum = psum.tile([P, N_TILE], F32, tag="flipped")
                nc.tensor.matmul(out=xb_sum[:], lhsT=ident_bf16[:], rhs=x_all[:, j, cols], start=True, stop=False)
                nc.tensor.matmul(out=xb_sum[:], lhsT=row_selector(0), rhs=vector_rows[:, cols], start=False, stop=True)
                sums.append(xb_sum)
            live["xb_sums", j] = sums

        def copy_biased(j, banks=range(D // N_TILE)):
            if ("xb", j) not in live:
                xb = work.tile([P, D], F32, tag="xb")
                live["xb", j] = xb
            for n in banks:
                nc.scalar.copy(out=live["xb", j][:, n * N_TILE : (n + 1) * N_TILE], in_=live["xb_sums", j][n][:])

        def project(j):
            codes, scales = live.pop(("o_mx", j))
            sums = []
            for n in range(D // N_TILE):
                acc = psum.tile([P, N_TILE], F32, tag="acc")
                mx_group(acc, codes, scales, wo_codes, wo_scales, slice(n * N_TILE, (n + 1) * N_TILE))
                sums.append(acc)
            live["attn", j] = sums

        def add_residual(j):
            xb = live.pop(("xb", j))
            residual = work.tile([P, D], F32, tag="residual")
            row_sums = work.tile([P, D // N_TILE], F32, tag="row_sums")
            for n, acc in enumerate(live.pop(("attn", j))):
                cols = slice(n * N_TILE, (n + 1) * N_TILE)
                nc.vector.scalar_tensor_tensor(
                    out=residual[:, cols], in0=acc[:], scalar=1.0, in1=xb[:, cols],
                    op0=ALU.mult, op1=ALU.add, accum_out=row_sums[:, n : n + 1],
                )
            live["residual", j] = residual
            live["row_sums", j] = row_sums

        def mean(j):
            parts = work.tile([P, D // N_TILE], F32, tag="mean_parts")
            neg_mean = work.tile([P, 1], F32, tag="neg_mean")
            nc.scalar.activation(
                out=parts[:], in_=live.pop(("row_sums", j))[:], func=ACT.Copy, scale=-1.0 / D, accum_out=neg_mean[:]
            )
            live["neg_mean", j] = neg_mean

        def sum_squares(j):
            squares = work.tile([P, D], BF16, tag="squares", bufs=1)
            sum_sq = work.tile([P, 1], F32, tag="sum_sq")
            nc.scalar.activation(
                out=squares[:], in_=live["residual", j][:], func=ACT.Square,
                bias=live["neg_mean", j][:], scale=1.0, accum_out=sum_sq[:],
            )
            live["sum_sq", j] = sum_sq

        def centre(j):
            centred = work.tile([P, D], F32, tag="centred")
            nc.vector.scalar_tensor_tensor(
                out=centred[:], in0=live.pop(("residual", j))[:], scalar=live.pop(("neg_mean", j))[:],
                in1=gamma_all[:], op0=ALU.add, op1=ALU.mult,
            )
            live["centred", j] = centred

        def inverse_std(j):
            var_eps = work.tile([P, 1], F32, tag="var_eps")
            nc.gpsimd.tensor_scalar(
                out=var_eps[:], in0=live.pop(("sum_sq", j))[:], scalar1=1.0 / D, scalar2=EPS,
                op0=ALU.mult, op1=ALU.add,
            )
            rstd = work.tile([P, 1], F32, tag="rstd")
            nc.gpsimd.tensor_tensor(out=rstd[:], in0=var_eps[:], in1=neg_half[:], op=ALU.pow)
            live["rstd", j] = rstd

        def normalise(j):
            xn = work.tile([P, D], F32, tag="xn", bufs=3)
            nc.vector.scalar_tensor_tensor(
                out=xn[:], in0=live.pop(("centred", j))[:], scalar=live.pop(("rstd", j))[:],
                in1=beta_all[:], op0=ALU.mult, op1=ALU.add,
            )
            nc.sync.dma_start(out=xn_tiles[j], in_=xn[:])
            live["xn", j] = xn

        def flip_normed(j):
            xn = live.pop(("xn", j))
            live["xn_flipped", j] = []
            for g in range(PASSES):
                flipped = psum.tile([P, PACK, P], F32, tag="flipped")
                for t in range(PACK):
                    k0 = g * K_PASS + t * P
                    nc.tensor.transpose(flipped[:, t, :], xn[:, k0 : k0 + P], ident_f32[:])
                live["xn_flipped", j].append(flipped)

        def copy_normed(j, copies=(nc.scalar.copy, nc.scalar.copy)):
            grouped = work.tile([P, D], BF16, align_bytes=64, tag="xn_grouped")
            for g, flipped in enumerate(live.pop(("xn_flipped", j))):
                copies[g](
                    out=grouped[:, g * K_PASS : (g + 1) * K_PASS].rearrange("p (r t) -> p r t", t=PACK),
                    in_=flipped[:].rearrange("p t r -> p r t"),
                )
            live["xn_grouped", j] = grouped

        def quantise_normed(j):
            grouped = live.pop(("xn_grouped", j))
            codes = work.tile([P, PASSES * P], U32, align_bytes=64, tag="xn_codes", bufs=LAG + 1)
            scales = work.tile([P, PASSES * P], U8, align_bytes=64, tag="xn_scales", bufs=LAG + 1)
            nc.vector.quantize_mx(out=codes[:].bitcast(FP8X4), scales=scales[:], in_=grouped[:])
            live["xn_mx", j] = (codes, scales)

        def hidden_matmuls(j, first):
            codes, scales = live["xn_mx", j] if first == 0 else live.pop(("xn_mx", j))
            sums = []
            for n in range(HALF // N_TILE):
                acc = psum.tile([P, N_TILE], F32, tag="acc")
                start = first + n * N_TILE
                mx_group(acc, codes, scales, w1_codes, w1_scales, slice(start, start + N_TILE))
                sums.append(acc)
            live["hidden_sums", j, first] = sums

        def add_hidden_bias(j, first, banks=range(HALF // N_TILE)):
            if ("hidden", j) not in live:
                hidden = work.tile([P, F], F32, tag="hidden", bufs=3)
                live["hidden", j] = hidden
            hidden = live["hidden", j]
            for n in banks:
                acc = live["hidden_sums", j, first][n]
                start = first + n * N_TILE
                nc.vector.tensor_tensor(
                    out=hidden[:, start : start + N_TILE], in0=acc[:],
                    in1=b1_all[:, start : start + N_TILE], op=ALU.add,
                )

        def gelu_store(j, first, width=HALF, last=None):
            last = first + HALF if last is None else last
            hidden = live["hidden", j]
            for c in range(first, last, width):
                piece = hidden[:, c : c + width]
                nc.scalar.activation(out=piece, in_=piece, func=ACT.Gelu)
                nc.sync.dma_start(out=h_tiles[j][:, c : c + width], in_=piece)

        def in_range(stage, j, *args):
            if 0 <= j < TOKEN_TILES:
                stage(j, *args)

        flip_heads(0)
        copy_heads(0)
        wo00 = regroup(wo_rows, 0, 0, nc.vector.tensor_copy)
        wo01 = regroup(wo_rows, 0, 1, nc.vector.tensor_copy)
        quantise(wo00, wo_codes, wo_scales)
        quantise(wo01, wo_codes, wo_scales)
        wo10 = regroup(wo_rows, 1, 0, (nc.vector.tensor_copy, nc.scalar.copy))
        spread_row(1, nc.scalar.copy, gamma_all)
        spread_row(2, nc.scalar.copy, beta_all)
        quantise_heads(0)
        wo11 = regroup(wo_rows, 1, 1, nc.vector.tensor_copy)
        quantise(wo10, wo_codes, wo_scales)
        quantise(wo11, wo_codes, wo_scales)
        bias_residual(0)
        copy_biased(0)
        project(0)

        pieces = {}
        pieces[0, 0] = regroup(w1_rows, 0, 0, nc.vector.tensor_copy)
        pieces[0, 1] = regroup(w1_rows, 0, 1, nc.scalar.copy)
        flip_heads(1)
        add_residual(0)
        mean(0)
        copy_heads(1)
        sum_squares(0)
        inverse_std(0)
        quantise(pieces.pop((0, 0)), w1_codes, w1_scales)
        centre(0)
        quantise_heads(1)
        pieces[1, 0] = regroup(w1_rows, 1, 0, nc.vector.tensor_copy)
        bias_residual(1)
        copy_biased(1)
        project(1)
        quantise(pieces.pop((0, 1)), w1_codes, w1_scales)
        quantise(pieces.pop((1, 0)), w1_codes, w1_scales)
        pieces[1, 1] = regroup(w1_rows, 1, 1, nc.scalar.copy)
        flip_heads(2)
        copy_heads(2)
        bias_residual(2)

        PLAN_V = {1: [(0,2),(1,2)]}
        PLAN_S = {1: [(0,3),(1,3)]}
        PLAN_QA = {1: [(1,1),(0,2),(1,2)]}
        PLAN_Q = {}
        PLAN_Q0 = {2: [(0,3),(1,3)]}
        for i in range(1, TOKEN_TILES - 1):
            in_range(add_residual, i)
            in_range(quantise_heads, i + 1)
            in_range(mean, i)
            in_range(copy_biased, i + 1, [0])
            in_range(sum_squares, i)
            in_range(inverse_std, i)
            in_range(copy_biased, i + 1, [1])
            in_range(normalise, i - 1)
            for name in PLAN_Q0.get(i, []):
                quantise(pieces.pop(name), w1_codes, w1_scales)
            in_range(hidden_matmuls, i - LAG, HALF)
            in_range(flip_normed, i - 1)
            in_range(copy_normed, i - 1)
            in_range(flip_heads, i + 2)
            in_range(copy_heads, i + 2)
            in_range(add_hidden_bias, i - LAG, 0)
            in_range(project, i + 1)
            in_range(bias_residual, i + 2)
            in_range(add_hidden_bias, i - LAG, HALF)
            in_range(centre, i)
            for g, n in PLAN_V.get(i, []):
                pieces[g, n] = regroup(w1_rows, g, n, nc.vector.tensor_copy)
            in_range(gelu_store, i - LAG, 0, F, F)
            for g, n in PLAN_S.get(i, []):
                pieces[g, n] = regroup(w1_rows, g, n, nc.scalar.copy)
            for name in PLAN_QA.get(i, []):
                quantise(pieces.pop(name), w1_codes, w1_scales)
            in_range(quantise_normed, i - 1)
            for name in PLAN_Q.get(i, []):
                quantise(pieces.pop(name), w1_codes, w1_scales)
            in_range(hidden_matmuls, i - LAG + 1, 0)

        j = TOKEN_TILES - 1
        add_residual(j)
        mean(j)
        sum_squares(j)
        inverse_std(j)
        normalise(j - 1)
        flip_normed(j - 1)
        copy_normed(j - 1)
        hidden_matmuls(j - 2, HALF)
        add_hidden_bias(j - 2, 0)
        centre(j)
        gelu_store(j - 2, 0)
        quantise_normed(j - 1)
        hidden_matmuls(j - 1, 0)
        add_hidden_bias(j - 2, HALF, [0])
        gelu_store(j - 2, HALF, N_TILE, HALF + N_TILE)
        normalise(j)
        flip_normed(j)
        add_hidden_bias(j - 2, HALF, [1])
        hidden_matmuls(j - 1, HALF)
        gelu_store(j - 2, HALF + N_TILE, N_TILE, F)
        add_hidden_bias(j - 1, 0)
        copy_normed(j, (nc.scalar.copy, nc.vector.tensor_copy))
        gelu_store(j - 1, 0)
        quantise_normed(j)
        hidden_matmuls(j, 0)
        add_hidden_bias(j - 1, HALF)
        gelu_store(j - 1, HALF, N_TILE)
        hidden_matmuls(j, HALF)
        add_hidden_bias(j, 0)
        gelu_store(j, 0, N_TILE)
        add_hidden_bias(j, HALF)
        gelu_store(j, HALF, N_TILE)
